import numpy as np
import ml_dtypes


def mxq(x, axis, fmt="e4m3"):
    dtype, down = {"e4m3": (ml_dtypes.float8_e4m3fn, 7), "e5m2": (ml_dtypes.float8_e5m2, 14)}[fmt]
    v = np.moveaxis(np.asarray(x, np.float32).astype(ml_dtypes.bfloat16).astype(np.float64), axis, -1)
    blocks = v.reshape(v.shape[:-1] + (-1, 32))
    amax = np.abs(blocks).max(-1, keepdims=True)
    byte = np.maximum(np.where(amax > 0, np.frexp(amax)[1] - 1 + 127, 0) - down, 1)
    scale = np.exp2(byte - 127.0)
    codes = (blocks / scale).astype(np.float32).astype(dtype).astype(np.float64)
    return np.moveaxis((codes * scale).reshape(v.shape), -1, axis)


BF16 = ml_dtypes.bfloat16


def bf(x):
    return np.asarray(x, np.float32).astype(BF16)


def f64(x):
    return np.asarray(x).astype(np.float64)


B, C, HI, WI, H_BINS = 128, 3, 64, 128, 64
EPS = 1e-6
SIGMA = 0.02


def setup_inputs():
    return {"x": bf(np.random.uniform(-0.25, 1.25, (B, C, HI, WI)))}


def reference(x):
    x = np.clip(f64(x), 0.0, 1.0)
    I = x[:, :C].reshape(B, C, -1).transpose(0, 2, 1)
    s = np.sum(I, axis=-1) + EPS
    Ir = I[:, :, 0] / s
    Ig = I[:, :, 1] / s
    bins = np.linspace(0.0, 1.0, H_BINS)
    kr = 1.0 / (1.0 + ((Ir[:, :, None] - bins) / SIGMA) ** 2)
    kg = 1.0 / (1.0 + ((Ig[:, :, None] - bins) / SIGMA) ** 2)
    krq = mxq(kr, 1, "e4m3")
    kgq = mxq(kg, 1, "e4m3")
    hists = (krq.transpose(0, 2, 1) @ kgq)[:, None, :, :]
    norm = np.sum(hists, axis=(1, 2, 3), keepdims=True) + EPS
    return hists / norm

@@ -1,0 +1,189 @@
+from contextlib import ExitStack
+
+import concourse.mybir as mybir
+
+F32 = mybir.dt.float32
+BF16 = mybir.dt.bfloat16
+I32 = mybir.dt.int32
+U32 = mybir.dt.uint32
+U8 = mybir.dt.uint8
+FP8X4 = mybir.dt.float8_e4m3fn_x4
+ALU = mybir.AluOpType
+ACT = mybir.ActivationFunctionType
+
+P = 128
+IMAGES = 128
+CHANNELS = 3
+PIXELS = 64 * 128
+BINS = 64
+EPS = 1e-6
+SIGMA = 0.02
+BIN_STEP = 1.0 / ((BINS - 1) * SIGMA)
+
+PACK = 4
+RUN = PIXELS // P
+PASSES = RUN // PACK
+COLS = 2 * BINS
+LANES = PASSES * 2 * PACK
+HALF_PASSES = PASSES // 2
+GROUP = 8
+
+SCALAR_BINS = 46
+
+FLOPS = 2 * IMAGES * PIXELS * BINS * BINS
+
+
+def tile_rgchromahistblock_k_kernel(tc, x, out):
+    nc = tc.nc
+    with ExitStack() as pools:
+        const = pools.enter_context(tc.tile_pool(name="const", bufs=1))
+        inputs = pools.enter_context(tc.tile_pool(name="inputs", bufs=2))
+        chroma_work = pools.enter_context(tc.tile_pool(name="chroma_work", bufs=1))
+        shifts = pools.enter_context(tc.tile_pool(name="shifts", bufs=2))
+        wide = pools.enter_context(tc.tile_pool(name="wide", bufs=4))
+        packed = pools.enter_context(tc.tile_pool(name="packed", bufs=3))
+        results = pools.enter_context(tc.tile_pool(name="results", bufs=2))
+        banks = pools.enter_context(tc.psum_pool(name="banks", bufs=2))
+
+        bin_number = const.tile([P, BINS], I32)
+        nc.gpsimd.iota(bin_number[:], pattern=[[1, BINS]], base=0, channel_multiplier=0)
+        centre = const.tile([P, BINS], F32)
+        nc.vector.tensor_scalar_mul(out=centre[:], in0=bin_number[:], scalar1=BIN_STEP)
+        one = const.tile([P, 1], F32)
+        nc.vector.memset(one[:], 1.0)
+        top_ones = const.tile([P, P], F32)
+        nc.vector.memset(top_ones[:], 0.0)
+        nc.vector.memset(top_ones[0:BINS, :], 1.0)
+        warm = const.tile([P, 1], F32)
+        nc.scalar.activation(out=warm[:], in_=one[:], func=ACT.Abs_reciprocal_sqrt, bias=one[:], scale=1.0)
+
+        shift_of = {}
+        wide_of = {}
+        bank_of = {}
+        result_of = {}
+
+        def chroma(group):
+            first = group * GROUP
+            raw = inputs.tile([P, GROUP, CHANNELS, RUN], BF16)
+            nc.sync.dma_start(
+                out=raw[:], in_=x[first : first + GROUP].rearrange("b c h (t q) -> (h t) b c q", q=RUN)
+            )
+            clipped = chroma_work.tile([P, GROUP, CHANNELS, RUN], F32)
+            nc.vector.tensor_scalar(
+                out=clipped[:], in0=raw[:], scalar1=0.0, scalar2=1.0, op0=ALU.max, op1=ALU.min
+            )
+            total = chroma_work.tile([P, GROUP, RUN], F32)
+            nc.vector.tensor_tensor(out=total[:], in0=clipped[:, :, 0, :], in1=clipped[:, :, 1, :], op=ALU.add)
+            nc.vector.scalar_tensor_tensor(
+                out=total[:], in0=clipped[:, :, 2, :], scalar=EPS, in1=total[:], op0=ALU.add, op1=ALU.add
+            )
+            inverse = chroma_work.tile([P, GROUP, RUN], F32)
+            nc.vector.reciprocal(out=inverse[:], in_=total[:])
+            shift = shifts.tile([P, GROUP, PASSES, 2, PACK], F32)
+            for channel in range(2):
+                nc.vector.scalar_tensor_tensor(
+                    out=shift[:, :, :, channel, :],
+                    in0=clipped[:, :, channel, :].rearrange("p b (c j) -> p b c j", j=PACK),
+                    scalar=-1.0 / SIGMA,
+                    in1=inverse[:].rearrange("p b (c j) -> p b c j", j=PACK),
+                    op0=ALU.mult,
+                    op1=ALU.mult,
+                )
+            shift_of[group] = shift
+
+        def squares(image):
+            shift = shift_of[image // GROUP]
+            lanes = shift[:, image % GROUP].rearrange("p c h j -> p (c h j)")
+            field = wide.tile([P, BINS, LANES], F32)
+            for w in range(SCALAR_BINS):
+                nc.scalar.activation(
+                    out=field[:, w, :], in_=lanes, func=ACT.Square, bias=centre[:, w : w + 1], scale=1.0
+                )
+            for w in range(SCALAR_BINS, BINS):
+                nc.vector.tensor_scalar_add(out=field[:, w, :], in0=lanes, scalar1=centre[:, w : w + 1])
+            rest = field[:, SCALAR_BINS:BINS, :].rearrange("p w l -> p (w l)")
+            nc.vector.tensor_tensor(out=rest, in0=rest, in1=rest, op=ALU.mult)
+            wide_of[image] = field
+
+        def inverse_roots(image):
+            field = wide_of[image]
+            for part in (field[:, 0:SCALAR_BINS, :], field[:, SCALAR_BINS:BINS, :]):
+                flat = part.rearrange("p w l -> p (w l)")
+                nc.scalar.activation(out=flat, in_=flat, func=ACT.Abs_reciprocal_sqrt, bias=one[:], scale=1.0)
+
+        def products(image):
+            field = wide_of[image]
+            bank = banks.tile([P, COLS], F32)
+            bank_of[image] = bank
+            halves = []
+            for half in range(2):
+                values = packed.tile([P, HALF_PASSES * 2, BINS, PACK], BF16, align_bytes=64)
+                roots = field[:].rearrange("p w (g j) -> p g w j", j=PACK)[
+                    :, half * HALF_PASSES * 2 : (half + 1) * HALF_PASSES * 2
+                ]
+                nc.vector.tensor_tensor(out=values[:], in0=roots, in1=roots, op=ALU.mult)
+                halves.append(values)
+            for half in range(2):
+                codes = packed.tile([P, HALF_PASSES * COLS], U32, align_bytes=64)
+                scales = packed.tile([P, HALF_PASSES * COLS], U8, align_bytes=64)
+                nc.vector.quantize_mx(
+                    out=codes[:].bitcast(FP8X4),
+                    scales=scales[:],
+                    in_=halves[half][:].rearrange("p g w j -> p (g w j)"),
+                )
+                for c in range(HALF_PASSES):
+                    cols = slice(c * COLS, (c + 1) * COLS)
+                    nc.tensor.matmul_mx(
+                        out=bank[:],
+                        lhsT=codes[:, cols].bitcast(FP8X4),
+                        lhsT_scale=scales[:, cols],
+                        rhs=codes[:, cols].bitcast(FP8X4),
+                        rhs_scale=scales[:, cols],
+                        start=(half == 0 and c == 0),
+                        stop=(half == 1 and c == HALF_PASSES - 1),
+                    )
+
+        def collect(image):
+            group = image // GROUP
+            if image % GROUP == 0:
+                hist = results.tile([P, GROUP, BINS], F32)
+                row_sums = results.tile([P, GROUP], F32)
+                result_of[group] = (hist, row_sums)
+            hist, row_sums = result_of[group]
+            b = image % GROUP
+            bank = bank_of[image]
+            nc.scalar.activation(
+                out=hist[:, b, :], in_=bank[:, BINS:COLS], func=ACT.Copy, accum_out=row_sums[:, b : b + 1]
+            )
+
+        def normalise(group):
+            hist, row_sums = result_of[group]
+            sums = banks.tile([P, GROUP], F32)
+            nc.tensor.matmul(out=sums[:], lhsT=top_ones[:], rhs=row_sums[:], start=True, stop=True)
+            divisor = results.tile([P, GROUP], F32)
+            nc.vector.tensor_scalar_add(out=divisor[:], in0=sums[:], scalar1=EPS)
+            factor = results.tile([P, GROUP], F32)
+            nc.vector.reciprocal(out=factor[:], in_=divisor[:])
+            normal = results.tile([P, GROUP, BINS], F32)
+            nc.vector.tensor_tensor(
+                out=normal[:], in0=hist[:], in1=factor[:].unsqueeze(2).to_broadcast([P, GROUP, BINS]), op=ALU.mult
+            )
+            first = group * GROUP
+            nc.sync.dma_start(
+                out=out[first : first + GROUP].rearrange("b o i j -> i (b o) j"), in_=normal[0:BINS]
+            )
+
+        chroma(0)
+        for step in range(IMAGES + 3):
+            if step % GROUP == 0 and step + GROUP < IMAGES:
+                chroma(step // GROUP + 1)
+            if step < IMAGES:
+                squares(step)
+            if 3 <= step:
+                collect(step - 3)
+            if 1 <= step <= IMAGES:
+                inverse_roots(step - 1)
+            if 2 <= step <= IMAGES + 1:
+                products(step - 2)
+            if 3 <= step and (step - 3) % GROUP == GROUP - 1:
+                normalise((step - 3) // GROUP)

@@ -27,6 +27,7 @@ COLS = 2 * BINS
 LANES = PASSES * 2 * PACK
 HALF_PASSES = PASSES // 2
 GROUP = 8
+COPIES = 4
 
 SCALAR_BINS = 46
 
@@ -59,6 +60,7 @@ def tile_rgchromahistblock_k_kernel(tc, x, out):
 
         shift_of = {}
         wide_of = {}
+        grouped_of = {}
         bank_of = {}
         result_of = {}
 
@@ -79,31 +81,48 @@ def tile_rgchromahistblock_k_kernel(tc, x, out):
             )
             inverse = chroma_work.tile([P, GROUP, RUN], F32)
             nc.vector.reciprocal(out=inverse[:], in_=total[:])
-            shift = shifts.tile([P, GROUP, PASSES, 2, PACK], F32)
+            shift = shifts.tile([P, COPIES, GROUP, PASSES, 2, PACK], F32)
             for channel in range(2):
                 nc.vector.scalar_tensor_tensor(
-                    out=shift[:, :, :, channel, :],
+                    out=shift[:, 0, :, :, channel, :],
                     in0=clipped[:, :, channel, :].rearrange("p b (c j) -> p b c j", j=PACK),
                     scalar=-1.0 / SIGMA,
                     in1=inverse[:].rearrange("p b (c j) -> p b c j", j=PACK),
                     op0=ALU.mult,
                     op1=ALU.mult,
                 )
+            for m in range(1, COPIES):
+                nc.vector.tensor_scalar_add(
+                    out=shift[:, m].rearrange("p b c h j -> p (b c h j)"),
+                    in0=shift[:, 0].rearrange("p b c h j -> p (b c h j)"),
+                    scalar1=m * BIN_STEP,
+                )
             shift_of[group] = shift
+
+        def bin_runs(first, last):
+            return [(w, min(COPIES, last - w)) for w in range(first, last, COPIES)]
 
         def squares(image):
             shift = shift_of[image // GROUP]
-            lanes = shift[:, image % GROUP].rearrange("p c h j -> p (c h j)")
+            lanes = shift[:, :, image % GROUP].rearrange("p m c h j -> p m (c h j)")
             field = wide.tile([P, BINS, LANES], F32)
-            for w in range(SCALAR_BINS):
+            for w, n in bin_runs(0, SCALAR_BINS):
                 nc.scalar.activation(
-                    out=field[:, w, :], in_=lanes, func=ACT.Square, bias=centre[:, w : w + 1], scale=1.0
+                    out=field[:, w : w + n, :],
+                    in_=lanes[:, 0:n, :],
+                    func=ACT.Square,
+                    bias=centre[:, w : w + 1],
+                    scale=1.0,
                 )
-            for w in range(SCALAR_BINS, BINS):
-                nc.vector.tensor_scalar_add(out=field[:, w, :], in0=lanes, scalar1=centre[:, w : w + 1])
-            rest = field[:, SCALAR_BINS:BINS, :].rearrange("p w l -> p (w l)")
-            nc.vector.tensor_tensor(out=rest, in0=rest, in1=rest, op=ALU.mult)
+            for w, n in bin_runs(SCALAR_BINS, BINS):
+                nc.vector.tensor_scalar_add(
+                    out=field[:, w : w + n, :], in0=lanes[:, 0:n, :], scalar1=centre[:, w : w + 1]
+                )
             wide_of[image] = field
+
+        def finish_squares(image):
+            rest = wide_of[image][:, SCALAR_BINS:BINS, :].rearrange("p w l -> p (w l)")
+            nc.vector.tensor_tensor(out=rest, in0=rest, in1=rest, op=ALU.mult)
 
         def inverse_roots(image):
             field = wide_of[image]
@@ -111,37 +130,38 @@ def tile_rgchromahistblock_k_kernel(tc, x, out):
                 flat = part.rearrange("p w l -> p (w l)")
                 nc.scalar.activation(out=flat, in_=flat, func=ACT.Abs_reciprocal_sqrt, bias=one[:], scale=1.0)
 
-        def products(image):
-            field = wide_of[image]
-            bank = banks.tile([P, COLS], F32)
-            bank_of[image] = bank
-            halves = []
-            for half in range(2):
-                values = packed.tile([P, HALF_PASSES * 2, BINS, PACK], BF16, align_bytes=64)
-                roots = field[:].rearrange("p w (g j) -> p g w j", j=PACK)[
-                    :, half * HALF_PASSES * 2 : (half + 1) * HALF_PASSES * 2
-                ]
-                nc.vector.tensor_tensor(out=values[:], in0=roots, in1=roots, op=ALU.mult)
-                halves.append(values)
-            for half in range(2):
-                codes = packed.tile([P, HALF_PASSES * COLS], U32, align_bytes=64)
-                scales = packed.tile([P, HALF_PASSES * COLS], U8, align_bytes=64)
-                nc.vector.quantize_mx(
-                    out=codes[:].bitcast(FP8X4),
-                    scales=scales[:],
-                    in_=halves[half][:].rearrange("p g w j -> p (g w j)"),
+        def values(image, half):
+            groups = HALF_PASSES * 2
+            grouped = packed.tile([P, groups, BINS, PACK], BF16, align_bytes=64)
+            roots = wide_of[image][:].rearrange("p w (g j) -> p g w j", j=PACK)[
+                :, half * groups : (half + 1) * groups
+            ]
+            nc.vector.tensor_tensor(out=grouped[:], in0=roots, in1=roots, op=ALU.mult)
+            grouped_of[(image, half)] = grouped
+
+        def multiply(image, half):
+            if half == 0:
+                bank = banks.tile([P, COLS], F32)
+                bank_of[image] = bank
+            bank = bank_of[image]
+            codes = packed.tile([P, HALF_PASSES * COLS], U32, align_bytes=64)
+            scales = packed.tile([P, HALF_PASSES * COLS], U8, align_bytes=64)
+            nc.vector.quantize_mx(
+                out=codes[:].bitcast(FP8X4),
+                scales=scales[:],
+                in_=grouped_of[(image, half)][:].rearrange("p g w j -> p (g w j)"),
+            )
+            for c in range(HALF_PASSES):
+                cols = slice(c * COLS, (c + 1) * COLS)
+                nc.tensor.matmul_mx(
+                    out=bank[:],
+                    lhsT=codes[:, cols].bitcast(FP8X4),
+                    lhsT_scale=scales[:, cols],
+                    rhs=codes[:, cols].bitcast(FP8X4),
+                    rhs_scale=scales[:, cols],
+                    start=(half == 0 and c == 0),
+                    stop=(half == 1 and c == HALF_PASSES - 1),
                 )
-                for c in range(HALF_PASSES):
-                    cols = slice(c * COLS, (c + 1) * COLS)
-                    nc.tensor.matmul_mx(
-                        out=bank[:],
-                        lhsT=codes[:, cols].bitcast(FP8X4),
-                        lhsT_scale=scales[:, cols],
-                        rhs=codes[:, cols].bitcast(FP8X4),
-                        rhs_scale=scales[:, cols],
-                        start=(half == 0 and c == 0),
-                        stop=(half == 1 and c == HALF_PASSES - 1),
-                    )
 
         def collect(image):
             group = image // GROUP
@@ -174,16 +194,23 @@ def tile_rgchromahistblock_k_kernel(tc, x, out):
             )
 
         chroma(0)
-        for step in range(IMAGES + 3):
+        for step in range(IMAGES + 5):
             if step % GROUP == 0 and step + GROUP < IMAGES:
                 chroma(step // GROUP + 1)
             if step < IMAGES:
                 squares(step)
-            if 3 <= step:
+            if 2 <= step <= IMAGES + 1:
+                values(step - 2, 0)
+            if step < IMAGES:
+                finish_squares(step)
+            if 2 <= step <= IMAGES + 1:
+                values(step - 2, 1)
+            if 3 <= step <= IMAGES + 2:
                 collect(step - 3)
             if 1 <= step <= IMAGES:
                 inverse_roots(step - 1)
             if 2 <= step <= IMAGES + 1:
-                products(step - 2)
-            if 3 <= step and (step - 3) % GROUP == GROUP - 1:
-                normalise((step - 3) // GROUP)
+                multiply(step - 2, 0)
+                multiply(step - 2, 1)
+            if 4 <= step and (step - 4) % GROUP == GROUP - 1:
+                normalise((step - 4) // GROUP)

@@ -29,7 +29,10 @@ HALF_PASSES = PASSES // 2
 GROUP = 8
 COPIES = 4
 
-SCALAR_BINS = 46
+RUNS = BINS // COPIES
+TRIPLES = RUNS // 3
+TRIPLE_BINS = TRIPLES * 3 * COPIES
+RUN_STEP = COPIES * BIN_STEP
 
 FLOPS = 2 * IMAGES * PIXELS * BINS * BINS
 
@@ -52,6 +55,8 @@ def tile_rgchromahistblock_k_kernel(tc, x, out):
         nc.vector.tensor_scalar_mul(out=centre[:], in0=bin_number[:], scalar1=BIN_STEP)
         one = const.tile([P, 1], F32)
         nc.vector.memset(one[:], 1.0)
+        one_derived = const.tile([P, 1], F32)
+        nc.vector.tensor_scalar_add(out=one_derived[:], in0=one[:], scalar1=2.0 * RUN_STEP * RUN_STEP)
         top_ones = const.tile([P, P], F32)
         nc.vector.memset(top_ones[:], 0.0)
         nc.vector.memset(top_ones[0:BINS, :], 1.0)
@@ -99,36 +104,37 @@ def tile_rgchromahistblock_k_kernel(tc, x, out):
                 )
             shift_of[group] = shift
 
-        def bin_runs(first, last):
-            return [(w, min(COPIES, last - w)) for w in range(first, last, COPIES)]
-
         def squares(image):
             shift = shift_of[image // GROUP]
             lanes = shift[:, :, image % GROUP].rearrange("p m c h j -> p m (c h j)")
             field = wide.tile([P, BINS, LANES], F32)
-            for w, n in bin_runs(0, SCALAR_BINS):
-                nc.scalar.activation(
-                    out=field[:, w : w + n, :],
-                    in_=lanes[:, 0:n, :],
-                    func=ACT.Square,
-                    bias=centre[:, w : w + 1],
-                    scale=1.0,
-                )
-            for w, n in bin_runs(SCALAR_BINS, BINS):
-                nc.vector.tensor_scalar_add(
-                    out=field[:, w : w + n, :], in0=lanes[:, 0:n, :], scalar1=centre[:, w : w + 1]
-                )
+            for run in range(RUNS):
+                w = run * COPIES
+                if run % 3 != 2:
+                    nc.scalar.activation(
+                        out=field[:, w : w + COPIES, :], in_=lanes, func=ACT.Square, bias=centre[:, w : w + 1], scale=1.0
+                    )
             wide_of[image] = field
 
-        def finish_squares(image):
-            rest = wide_of[image][:, SCALAR_BINS:BINS, :].rearrange("p w l -> p (w l)")
-            nc.vector.tensor_tensor(out=rest, in0=rest, in1=rest, op=ALU.mult)
+        def triples_of(field):
+            return field[:, 0:TRIPLE_BINS, :].rearrange("p (t r w) l -> p t r (w l)", r=3, w=COPIES)
+
+        def derive(image):
+            runs = triples_of(wide_of[image])
+            nc.vector.scalar_tensor_tensor(
+                out=runs[:, :, 2, :], in0=runs[:, :, 1, :], scalar=2.0, in1=runs[:, :, 0, :],
+                op0=ALU.mult, op1=ALU.subtract,
+            )
 
         def inverse_roots(image):
             field = wide_of[image]
-            for part in (field[:, 0:SCALAR_BINS, :], field[:, SCALAR_BINS:BINS, :]):
-                flat = part.rearrange("p w l -> p (w l)")
-                nc.scalar.activation(out=flat, in_=flat, func=ACT.Abs_reciprocal_sqrt, bias=one[:], scale=1.0)
+            runs = triples_of(field)
+            for part, offset in (
+                (runs[:, :, 0:2, :].rearrange("p t r e -> p t (r e)"), one),
+                (field[:, TRIPLE_BINS:BINS, :].rearrange("p w l -> p (w l)"), one),
+                (runs[:, :, 2, :], one_derived),
+            ):
+                nc.scalar.activation(out=part, in_=part, func=ACT.Abs_reciprocal_sqrt, bias=offset[:], scale=1.0)
 
         def values(image, half):
             groups = HALF_PASSES * 2
@@ -201,9 +207,6 @@ def tile_rgchromahistblock_k_kernel(tc, x, out):
                 squares(step)
             if 2 <= step <= IMAGES + 1:
                 values(step - 2, 0)
-            if step < IMAGES:
-                finish_squares(step)
-            if 2 <= step <= IMAGES + 1:
                 values(step - 2, 1)
             if 3 <= step <= IMAGES + 2:
                 collect(step - 3)
@@ -212,5 +215,7 @@ def tile_rgchromahistblock_k_kernel(tc, x, out):
             if 2 <= step <= IMAGES + 1:
                 multiply(step - 2, 0)
                 multiply(step - 2, 1)
+            if step < IMAGES:
+                derive(step)
             if 4 <= step and (step - 4) % GROUP == GROUP - 1:
                 normalise((step - 4) // GROUP)

@@ -1,6 +1,7 @@
 from contextlib import ExitStack
 
 import concourse.mybir as mybir
+from concourse.masks import make_identity
 
 F32 = mybir.dt.float32
 BF16 = mybir.dt.bfloat16
@@ -14,27 +15,39 @@ ACT = mybir.ActivationFunctionType
 P = 128
 IMAGES = 128
 CHANNELS = 3
-PIXELS = 64 * 128
+ROWS = 64
+WIDTH = 128
+PIXELS = ROWS * WIDTH
 BINS = 64
 EPS = 1e-6
 SIGMA = 0.02
-BIN_STEP = 1.0 / ((BINS - 1) * SIGMA)
+STEP = 1.0 / ((BINS - 1) * SIGMA)
+MIDDLE = (BINS - 1) / 2.0
 
 PACK = 4
-RUN = PIXELS // P
-PASSES = RUN // PACK
+PASSES = ROWS // PACK
 COLS = 2 * BINS
-LANES = PASSES * 2 * PACK
 HALF_PASSES = PASSES // 2
+PAIR = 2
+PAIRS = IMAGES // PAIR
+LOADED_PAIRS = 2
+LOADED = PAIR * LOADED_PAIRS
 GROUP = 8
-COPIES = 4
+LANES = 2 * PAIR * ROWS
 
-RUNS = BINS // COPIES
-TRIPLES = RUNS // 3
-TRIPLE_BINS = TRIPLES * 3 * COPIES
-RUN_STEP = COPIES * BIN_STEP
+REACH = 3
+SPAN = 2 * REACH + 1
+LOW_BASES = list(range(0, BINS // 2, SPAN))
+BASES = LOW_BASES + [BINS - 1 - base for base in LOW_BASES]
+OFFSETS = [-3, -2, -1, 1, 2, 3]
 
 FLOPS = 2 * IMAGES * PIXELS * BINS * BINS
+
+SCALAR_UNITS = 1
+
+
+def base_of(bin_number):
+    return (bin_number + REACH) // SPAN * SPAN
 
 
 def tile_rgchromahistblock_k_kernel(tc, x, out):
@@ -43,148 +56,183 @@ def tile_rgchromahistblock_k_kernel(tc, x, out):
         const = pools.enter_context(tc.tile_pool(name="const", bufs=1))
         inputs = pools.enter_context(tc.tile_pool(name="inputs", bufs=2))
         chroma_work = pools.enter_context(tc.tile_pool(name="chroma_work", bufs=1))
-        shifts = pools.enter_context(tc.tile_pool(name="shifts", bufs=2))
-        wide = pools.enter_context(tc.tile_pool(name="wide", bufs=4))
+        lanes_pool = pools.enter_context(tc.tile_pool(name="lanes_pool", bufs=2))
+        wide = pools.enter_context(tc.tile_pool(name="wide", bufs=3))
+        grouped_pool = pools.enter_context(tc.tile_pool(name="grouped_pool", bufs=4))
         packed = pools.enter_context(tc.tile_pool(name="packed", bufs=3))
         results = pools.enter_context(tc.tile_pool(name="results", bufs=2))
-        banks = pools.enter_context(tc.psum_pool(name="banks", bufs=2))
+        squares_banks = pools.enter_context(tc.psum_pool(name="squares_banks", bufs=5))
+        hist_banks = pools.enter_context(tc.psum_pool(name="hist_banks", bufs=2))
+        sum_banks = pools.enter_context(tc.psum_pool(name="sum_banks", bufs=1))
 
         bin_number = const.tile([P, BINS], I32)
         nc.gpsimd.iota(bin_number[:], pattern=[[1, BINS]], base=0, channel_multiplier=0)
         centre = const.tile([P, BINS], F32)
-        nc.vector.tensor_scalar_mul(out=centre[:], in0=bin_number[:], scalar1=BIN_STEP)
+        nc.vector.tensor_scalar_mul(out=centre[:], in0=bin_number[:], scalar1=STEP)
         one = const.tile([P, 1], F32)
         nc.vector.memset(one[:], 1.0)
-        one_derived = const.tile([P, 1], F32)
-        nc.vector.tensor_scalar_add(out=one_derived[:], in0=one[:], scalar1=2.0 * RUN_STEP * RUN_STEP)
+        identity = const.tile([P, P], F32)
+        make_identity(nc, identity[:])
+        rest = const.tile([P, BINS // 2], F32)
+        for j in range(BINS // 2):
+            t = (j - base_of(j)) * STEP
+            nc.gpsimd.tensor_scalar(
+                out=rest[:, j : j + 1], in0=one[:], scalar1=1.0 + 2.0 * t * (base_of(j) - MIDDLE) * STEP + t * t,
+                scalar2=0.0, op0=ALU.mult, op1=ALU.add,
+            )
         top_ones = const.tile([P, P], F32)
         nc.vector.memset(top_ones[:], 0.0)
         nc.vector.memset(top_ones[0:BINS, :], 1.0)
         warm = const.tile([P, 1], F32)
         nc.scalar.activation(out=warm[:], in_=one[:], func=ACT.Abs_reciprocal_sqrt, bias=one[:], scale=1.0)
 
-        shift_of = {}
-        wide_of = {}
+        minus_of = {}
+        base_of_pair = {}
+        slope_of_pair = {}
+        roots_of = {}
         grouped_of = {}
         bank_of = {}
         result_of = {}
 
-        def chroma(group):
-            first = group * GROUP
-            raw = inputs.tile([P, GROUP, CHANNELS, RUN], BF16)
-            nc.sync.dma_start(
-                out=raw[:], in_=x[first : first + GROUP].rearrange("b c h (t q) -> (h t) b c q", q=RUN)
-            )
-            clipped = chroma_work.tile([P, GROUP, CHANNELS, RUN], F32)
+        def image_of(pair, b):
+            return pair // LOADED_PAIRS * LOADED + b * LOADED_PAIRS + pair % LOADED_PAIRS
+
+        def chroma(load):
+            first = load * LOADED
+            raw = inputs.tile([P, LOADED_PAIRS, CHANNELS, WIDTH], BF16)
+            for b in range(PAIR):
+                start = first + b * LOADED_PAIRS
+                nc.sync.dma_start(
+                    out=raw[b * ROWS : (b + 1) * ROWS],
+                    in_=x[start : start + LOADED_PAIRS].rearrange("a c h w -> h a c w"),
+                )
+            clipped = chroma_work.tile([P, LOADED_PAIRS, CHANNELS, WIDTH], F32)
             nc.vector.tensor_scalar(
                 out=clipped[:], in0=raw[:], scalar1=0.0, scalar2=1.0, op0=ALU.max, op1=ALU.min
             )
-            total = chroma_work.tile([P, GROUP, RUN], F32)
+            total = chroma_work.tile([P, LOADED_PAIRS, WIDTH], F32)
             nc.vector.tensor_tensor(out=total[:], in0=clipped[:, :, 0, :], in1=clipped[:, :, 1, :], op=ALU.add)
             nc.vector.scalar_tensor_tensor(
                 out=total[:], in0=clipped[:, :, 2, :], scalar=EPS, in1=total[:], op0=ALU.add, op1=ALU.add
             )
-            inverse = chroma_work.tile([P, GROUP, RUN], F32)
+            inverse = chroma_work.tile([P, LOADED_PAIRS, WIDTH], F32)
             nc.vector.reciprocal(out=inverse[:], in_=total[:])
-            shift = shifts.tile([P, COPIES, GROUP, PASSES, 2, PACK], F32)
+            minus = lanes_pool.tile([P, LOADED_PAIRS, 2, WIDTH], F32)
             for channel in range(2):
                 nc.vector.scalar_tensor_tensor(
-                    out=shift[:, 0, :, :, channel, :],
-                    in0=clipped[:, :, channel, :].rearrange("p b (c j) -> p b c j", j=PACK),
-                    scalar=-1.0 / SIGMA,
-                    in1=inverse[:].rearrange("p b (c j) -> p b c j", j=PACK),
-                    op0=ALU.mult,
-                    op1=ALU.mult,
+                    out=minus[:, :, channel, :], in0=clipped[:, :, channel, :], scalar=-1.0 / SIGMA,
+                    in1=inverse[:], op0=ALU.mult, op1=ALU.mult,
                 )
-            for m in range(1, COPIES):
-                nc.vector.tensor_scalar_add(
-                    out=shift[:, m].rearrange("p b c h j -> p (b c h j)"),
-                    in0=shift[:, 0].rearrange("p b c h j -> p (b c h j)"),
-                    scalar1=m * BIN_STEP,
+            minus_of[load] = minus
+
+        def prepare(pair):
+            source = minus_of[pair // LOADED_PAIRS][:, pair % LOADED_PAIRS].rearrange("p g w -> p (g w)")
+            base = lanes_pool.tile([P, len(BASES), 2, WIDTH], F32)
+            slope = lanes_pool.tile([P, len(OFFSETS), 2, WIDTH], F32)
+            for i, t in enumerate(OFFSETS):
+                nc.vector.tensor_scalar(
+                    out=slope[:, i].rearrange("p g w -> p (g w)"), in0=source,
+                    scalar1=2.0 * t * STEP, scalar2=2.0 * t * STEP * MIDDLE * STEP, op0=ALU.mult, op1=ALU.add,
                 )
-            shift_of[group] = shift
+            for i, j in enumerate(BASES):
+                nc.scalar.activation(
+                    out=base[:, i].rearrange("p g w -> p (g w)"), in_=source,
+                    func=ACT.Square, bias=centre[:, j : j + 1], scale=1.0,
+                )
+            base_of_pair[pair] = base
+            slope_of_pair[pair] = slope
 
-        def squares(image):
-            shift = shift_of[image // GROUP]
-            lanes = shift[:, :, image % GROUP].rearrange("p m c h j -> p m (c h j)")
-            field = wide.tile([P, BINS, LANES], F32)
-            for run in range(RUNS):
-                w = run * COPIES
-                if run % 3 != 2:
-                    nc.scalar.activation(
-                        out=field[:, w : w + COPIES, :], in_=lanes, func=ACT.Square, bias=centre[:, w : w + 1], scale=1.0
-                    )
-            wide_of[image] = field
+        def roots(pair, half):
+            base = base_of_pair[pair]
+            slope = slope_of_pair[pair]
+            root = wide.tile([P, BINS // 2, LANES], F32)
+            for slot in range(BINS // 4):
+                j = half * BINS // 4 + slot
+                t = j - base_of(j)
+                bank = squares_banks.tile([P, 2, 2, P], F32)
+                for side in range(2):
+                    for channel in range(2):
+                        i = LOW_BASES.index(base_of(j)) + side * len(LOW_BASES)
+                        nc.tensor.matmul(
+                            out=bank[:, side, channel, :], lhsT=base[:, i, channel, :], rhs=identity[:],
+                            is_transpose=True, start=True, stop=(t == 0),
+                        )
+                        if t != 0:
+                            i = OFFSETS.index(t if side == 0 else -t)
+                            nc.tensor.matmul(
+                                out=bank[:, side, channel, :], lhsT=slope[:, i, channel, :], rhs=identity[:],
+                                is_transpose=True, start=False, stop=True,
+                            )
+                nc.scalar.activation(
+                    out=root[:, slot : BINS // 2 - slot : BINS // 2 - 1 - 2 * slot, :],
+                    in_=bank[:].rearrange("p s c l -> p s (c l)"),
+                    func=ACT.Abs_reciprocal_sqrt, bias=rest[:, j : j + 1], scale=1.0,
+                )
+            roots_of[(pair, half)] = root
 
-        def triples_of(field):
-            return field[:, 0:TRIPLE_BINS, :].rearrange("p (t r w) l -> p t r (w l)", r=3, w=COPIES)
-
-        def derive(image):
-            runs = triples_of(wide_of[image])
-            nc.vector.scalar_tensor_tensor(
-                out=runs[:, :, 2, :], in0=runs[:, :, 1, :], scalar=2.0, in1=runs[:, :, 0, :],
-                op0=ALU.mult, op1=ALU.subtract,
-            )
-
-        def inverse_roots(image):
-            field = wide_of[image]
-            runs = triples_of(field)
-            for part, offset in (
-                (runs[:, :, 0:2, :].rearrange("p t r e -> p t (r e)"), one),
-                (field[:, TRIPLE_BINS:BINS, :].rearrange("p w l -> p (w l)"), one),
-                (runs[:, :, 2, :], one_derived),
-            ):
-                nc.scalar.activation(out=part, in_=part, func=ACT.Abs_reciprocal_sqrt, bias=offset[:], scale=1.0)
-
-        def values(image, half):
-            groups = HALF_PASSES * 2
-            grouped = packed.tile([P, groups, BINS, PACK], BF16, align_bytes=64)
-            roots = wide_of[image][:].rearrange("p w (g j) -> p g w j", j=PACK)[
-                :, half * groups : (half + 1) * groups
-            ]
-            nc.vector.tensor_tensor(out=grouped[:], in0=roots, in1=roots, op=ALU.mult)
-            grouped_of[(image, half)] = grouped
-
-        def multiply(image, half):
+        def values(pair, half):
+            root = roots_of[(pair, half)]
             if half == 0:
-                bank = banks.tile([P, COLS], F32)
-                bank_of[image] = bank
-            bank = bank_of[image]
-            codes = packed.tile([P, HALF_PASSES * COLS], U32, align_bytes=64)
-            scales = packed.tile([P, HALF_PASSES * COLS], U8, align_bytes=64)
-            nc.vector.quantize_mx(
-                out=codes[:].bitcast(FP8X4),
-                scales=scales[:],
-                in_=grouped_of[(image, half)][:].rearrange("p g w j -> p (g w j)"),
-            )
-            for c in range(HALF_PASSES):
-                cols = slice(c * COLS, (c + 1) * COLS)
-                nc.tensor.matmul_mx(
-                    out=bank[:],
-                    lhsT=codes[:, cols].bitcast(FP8X4),
-                    lhsT_scale=scales[:, cols],
-                    rhs=codes[:, cols].bitcast(FP8X4),
-                    rhs_scale=scales[:, cols],
-                    start=(half == 0 and c == 0),
-                    stop=(half == 1 and c == HALF_PASSES - 1),
-                )
+                for b in range(PAIR):
+                    grouped = grouped_pool.tile([P, PASSES, 2, BINS, PACK], BF16, align_bytes=64)
+                    grouped_of[(pair, b)] = grouped
+            unit = half * 8
+            for b in range(PAIR):
+                grouped = grouped_of[(pair, b)]
+                for channel in range(2):
+                    for side in range(2):
+                        low = (0, BINS - 16)[side] if half == 0 else (16, 32)[side]
+                        lane = channel * P + b * ROWS
+                        source = root[:, side * 16 : side * 16 + 16, lane : lane + ROWS].rearrange(
+                            "p w (c j) -> p c w j", j=PACK
+                        )
+                        target = grouped[:, :, channel, low : low + 16, :]
+                        if unit < SCALAR_UNITS:
+                            nc.scalar.activation(out=target, in_=source, func=ACT.Square)
+                        else:
+                            nc.vector.tensor_tensor(out=target, in0=source, in1=source, op=ALU.mult)
+                        unit += 1
 
-        def collect(image):
+        def multiply(pair, b):
+            grouped = grouped_of[(pair, b)]
+            bank = hist_banks.tile([P, 512], F32)
+            bank_of[(pair, b)] = bank
+            for half in range(2):
+                codes = packed.tile([P, HALF_PASSES * COLS], U32, align_bytes=64)
+                scales = packed.tile([P, HALF_PASSES * COLS], U8, align_bytes=64)
+                nc.vector.quantize_mx(
+                    out=codes[:].bitcast(FP8X4),
+                    scales=scales[:],
+                    in_=grouped[:, half * HALF_PASSES : (half + 1) * HALF_PASSES].rearrange("p c g w j -> p (c g w j)"),
+                )
+                for c in range(HALF_PASSES):
+                    cols = slice(c * COLS, (c + 1) * COLS)
+                    nc.tensor.matmul_mx(
+                        out=bank[:, 0:COLS],
+                        lhsT=codes[:, cols].bitcast(FP8X4),
+                        lhsT_scale=scales[:, cols],
+                        rhs=codes[:, cols].bitcast(FP8X4),
+                        rhs_scale=scales[:, cols],
+                        start=(half == 0 and c == 0),
+                        stop=(half == 1 and c == HALF_PASSES - 1),
+                    )
+
+        def collect(pair, b):
+            image = image_of(pair, b)
             group = image // GROUP
-            if image % GROUP == 0:
+            if group not in result_of:
                 hist = results.tile([P, GROUP, BINS], F32)
                 row_sums = results.tile([P, GROUP], F32)
                 result_of[group] = (hist, row_sums)
             hist, row_sums = result_of[group]
-            b = image % GROUP
-            bank = bank_of[image]
+            i = image % GROUP
             nc.scalar.activation(
-                out=hist[:, b, :], in_=bank[:, BINS:COLS], func=ACT.Copy, accum_out=row_sums[:, b : b + 1]
+                out=hist[:, i, :], in_=bank_of[(pair, b)][:, BINS:COLS], func=ACT.Copy, accum_out=row_sums[:, i : i + 1]
             )
 
         def normalise(group):
             hist, row_sums = result_of[group]
-            sums = banks.tile([P, GROUP], F32)
+            sums = sum_banks.tile([P, GROUP], F32)
             nc.tensor.matmul(out=sums[:], lhsT=top_ones[:], rhs=row_sums[:], start=True, stop=True)
             divisor = results.tile([P, GROUP], F32)
             nc.vector.tensor_scalar_add(out=divisor[:], in0=sums[:], scalar1=EPS)
@@ -199,23 +247,25 @@ def tile_rgchromahistblock_k_kernel(tc, x, out):
                 out=out[first : first + GROUP].rearrange("b o i j -> i (b o) j"), in_=normal[0:BINS]
             )
 
+        pairs_of_group = GROUP // PAIR
         chroma(0)
-        for step in range(IMAGES + 5):
-            if step % GROUP == 0 and step + GROUP < IMAGES:
-                chroma(step // GROUP + 1)
-            if step < IMAGES:
-                squares(step)
-            if 2 <= step <= IMAGES + 1:
-                values(step - 2, 0)
-                values(step - 2, 1)
-            if 3 <= step <= IMAGES + 2:
-                collect(step - 3)
-            if 1 <= step <= IMAGES:
-                inverse_roots(step - 1)
-            if 2 <= step <= IMAGES + 1:
-                multiply(step - 2, 0)
-                multiply(step - 2, 1)
-            if step < IMAGES:
-                derive(step)
-            if 4 <= step and (step - 4) % GROUP == GROUP - 1:
-                normalise((step - 4) // GROUP)
+        prepare(0)
+        for step in range(PAIRS + 3):
+            if step < PAIRS:
+                roots(step, 0)
+            if 1 <= step <= PAIRS:
+                values(step - 1, 1)
+                multiply(step - 1, 0)
+                multiply(step - 1, 1)
+            if step % LOADED_PAIRS == 0 and step + LOADED_PAIRS < PAIRS:
+                chroma(step // LOADED_PAIRS + 1)
+            if step + 1 < PAIRS:
+                prepare(step + 1)
+            if step < PAIRS:
+                roots(step, 1)
+                values(step, 0)
+            if 1 <= step <= PAIRS:
+                collect(step - 1, 0)
+                collect(step - 1, 1)
+            if 2 <= step and (step - 2) % pairs_of_group == pairs_of_group - 1:
+                normalise((step - 2) // pairs_of_group)

@@ -58,8 +58,8 @@ def tile_rgchromahistblock_k_kernel(tc, x, out):
         chroma_work = pools.enter_context(tc.tile_pool(name="chroma_work", bufs=1))
         lanes_pool = pools.enter_context(tc.tile_pool(name="lanes_pool", bufs=2))
         wide = pools.enter_context(tc.tile_pool(name="wide", bufs=3))
-        grouped_pool = pools.enter_context(tc.tile_pool(name="grouped_pool", bufs=4))
-        packed = pools.enter_context(tc.tile_pool(name="packed", bufs=3))
+        grouped_pool = pools.enter_context(tc.tile_pool(name="grouped_pool", bufs=3))
+        packed = pools.enter_context(tc.tile_pool(name="packed", bufs=4))
         results = pools.enter_context(tc.tile_pool(name="results", bufs=2))
         squares_banks = pools.enter_context(tc.psum_pool(name="squares_banks", bufs=5))
         hist_banks = pools.enter_context(tc.psum_pool(name="hist_banks", bufs=2))
@@ -86,18 +86,21 @@ def tile_rgchromahistblock_k_kernel(tc, x, out):
         warm = const.tile([P, 1], F32)
         nc.scalar.activation(out=warm[:], in_=one[:], func=ACT.Abs_reciprocal_sqrt, bias=one[:], scale=1.0)
 
+        raw_of = {}
         minus_of = {}
         base_of_pair = {}
         slope_of_pair = {}
         roots_of = {}
         grouped_of = {}
         bank_of = {}
+        bank_of_squares = {}
+        packed_of = {}
         result_of = {}
 
         def image_of(pair, b):
             return pair // LOADED_PAIRS * LOADED + b * LOADED_PAIRS + pair % LOADED_PAIRS
 
-        def chroma(load):
+        def fetch(load):
             first = load * LOADED
             raw = inputs.tile([P, LOADED_PAIRS, CHANNELS, WIDTH], BF16)
             for b in range(PAIR):
@@ -106,6 +109,10 @@ def tile_rgchromahistblock_k_kernel(tc, x, out):
                     out=raw[b * ROWS : (b + 1) * ROWS],
                     in_=x[start : start + LOADED_PAIRS].rearrange("a c h w -> h a c w"),
                 )
+            raw_of[load] = raw
+
+        def chroma(load):
+            raw = raw_of[load]
             clipped = chroma_work.tile([P, LOADED_PAIRS, CHANNELS, WIDTH], F32)
             nc.vector.tensor_scalar(
                 out=clipped[:], in0=raw[:], scalar1=0.0, scalar2=1.0, op0=ALU.max, op1=ALU.min
@@ -125,78 +132,80 @@ def tile_rgchromahistblock_k_kernel(tc, x, out):
                 )
             minus_of[load] = minus
 
-        def prepare(pair):
-            source = minus_of[pair // LOADED_PAIRS][:, pair % LOADED_PAIRS].rearrange("p g w -> p (g w)")
-            base = lanes_pool.tile([P, len(BASES), 2, WIDTH], F32)
+        def source_of(pair):
+            return minus_of[pair // LOADED_PAIRS][:, pair % LOADED_PAIRS].rearrange("p g w -> p (g w)")
+
+        def slopes(pair):
             slope = lanes_pool.tile([P, len(OFFSETS), 2, WIDTH], F32)
             for i, t in enumerate(OFFSETS):
                 nc.vector.tensor_scalar(
-                    out=slope[:, i].rearrange("p g w -> p (g w)"), in0=source,
+                    out=slope[:, i].rearrange("p g w -> p (g w)"), in0=source_of(pair),
                     scalar1=2.0 * t * STEP, scalar2=2.0 * t * STEP * MIDDLE * STEP, op0=ALU.mult, op1=ALU.add,
                 )
-            for i, j in enumerate(BASES):
-                nc.scalar.activation(
-                    out=base[:, i].rearrange("p g w -> p (g w)"), in_=source,
-                    func=ACT.Square, bias=centre[:, j : j + 1], scale=1.0,
-                )
-            base_of_pair[pair] = base
             slope_of_pair[pair] = slope
 
-        def roots(pair, half):
+        def base_square(pair, i):
+            if i == 0:
+                base = lanes_pool.tile([P, len(BASES), 2, WIDTH], F32)
+                base_of_pair[pair] = base
+            base = base_of_pair[pair]
+            j = BASES[i]
+            nc.scalar.activation(
+                out=base[:, i].rearrange("p g w -> p (g w)"), in_=source_of(pair),
+                func=ACT.Square, bias=centre[:, j : j + 1], scale=1.0,
+            )
+
+        def squares(pair, half, slot):
             base = base_of_pair[pair]
             slope = slope_of_pair[pair]
-            root = wide.tile([P, BINS // 2, LANES], F32)
-            for slot in range(BINS // 4):
-                j = half * BINS // 4 + slot
-                t = j - base_of(j)
-                bank = squares_banks.tile([P, 2, 2, P], F32)
-                for side in range(2):
-                    for channel in range(2):
-                        i = LOW_BASES.index(base_of(j)) + side * len(LOW_BASES)
-                        nc.tensor.matmul(
-                            out=bank[:, side, channel, :], lhsT=base[:, i, channel, :], rhs=identity[:],
-                            is_transpose=True, start=True, stop=(t == 0),
-                        )
-                        if t != 0:
-                            i = OFFSETS.index(t if side == 0 else -t)
-                            nc.tensor.matmul(
-                                out=bank[:, side, channel, :], lhsT=slope[:, i, channel, :], rhs=identity[:],
-                                is_transpose=True, start=False, stop=True,
-                            )
-                nc.scalar.activation(
-                    out=root[:, slot : BINS // 2 - slot : BINS // 2 - 1 - 2 * slot, :],
-                    in_=bank[:].rearrange("p s c l -> p s (c l)"),
-                    func=ACT.Abs_reciprocal_sqrt, bias=rest[:, j : j + 1], scale=1.0,
-                )
-            roots_of[(pair, half)] = root
-
-        def values(pair, half):
-            root = roots_of[(pair, half)]
-            if half == 0:
-                for b in range(PAIR):
-                    grouped = grouped_pool.tile([P, PASSES, 2, BINS, PACK], BF16, align_bytes=64)
-                    grouped_of[(pair, b)] = grouped
-            unit = half * 8
-            for b in range(PAIR):
-                grouped = grouped_of[(pair, b)]
+            j = half * BINS // 4 + slot
+            t = j - base_of(j)
+            bank = squares_banks.tile([P, 2, 2, P], F32)
+            for side in range(2):
                 for channel in range(2):
-                    for side in range(2):
-                        low = (0, BINS - 16)[side] if half == 0 else (16, 32)[side]
-                        lane = channel * P + b * ROWS
-                        source = root[:, side * 16 : side * 16 + 16, lane : lane + ROWS].rearrange(
-                            "p w (c j) -> p c w j", j=PACK
+                    i = LOW_BASES.index(base_of(j)) + side * len(LOW_BASES)
+                    nc.tensor.matmul(
+                        out=bank[:, side, channel, :], lhsT=base[:, i, channel, :], rhs=identity[:],
+                        is_transpose=True, start=True, stop=(t == 0),
+                    )
+                    if t != 0:
+                        i = OFFSETS.index(t if side == 0 else -t)
+                        nc.tensor.matmul(
+                            out=bank[:, side, channel, :], lhsT=slope[:, i, channel, :], rhs=identity[:],
+                            is_transpose=True, start=False, stop=True,
                         )
-                        target = grouped[:, :, channel, low : low + 16, :]
-                        if unit < SCALAR_UNITS:
-                            nc.scalar.activation(out=target, in_=source, func=ACT.Square)
-                        else:
-                            nc.vector.tensor_tensor(out=target, in0=source, in1=source, op=ALU.mult)
-                        unit += 1
+            bank_of_squares[(pair, half, slot)] = bank
 
-        def multiply(pair, b):
+        def roots(pair, half, slot):
+            if slot == 0:
+                root = wide.tile([P, BINS // 2, LANES], F32)
+                roots_of[(pair, half)] = root
+            root = roots_of[(pair, half)]
+            j = half * BINS // 4 + slot
+            nc.scalar.activation(
+                out=root[:, slot : BINS // 2 - slot : BINS // 2 - 1 - 2 * slot, :],
+                in_=bank_of_squares[(pair, half, slot)][:].rearrange("p s c l -> p s (c l)"),
+                func=ACT.Abs_reciprocal_sqrt, bias=rest[:, j : j + 1], scale=1.0,
+            )
+
+        def values(pair, half, unit):
+            root = roots_of[(pair, half)]
+            b, channel, side = unit // 4, unit // 2 % 2, unit % 2
+            if half == 0 and (pair, b) not in grouped_of:
+                grouped = grouped_pool.tile([P, PASSES, 2, BINS, PACK], BF16, align_bytes=64)
+                grouped_of[(pair, b)] = grouped
             grouped = grouped_of[(pair, b)]
-            bank = hist_banks.tile([P, 512], F32)
-            bank_of[(pair, b)] = bank
+            low = (0, BINS - 16)[side] if half == 0 else (16, 32)[side]
+            lane = channel * P + b * ROWS
+            source = root[:, side * 16 : side * 16 + 16, lane : lane + ROWS].rearrange("p w (c j) -> p c w j", j=PACK)
+            target = grouped[:, :, channel, low : low + 16, :]
+            if half == 0 and unit < SCALAR_UNITS:
+                nc.scalar.activation(out=target, in_=source, func=ACT.Square)
+            else:
+                nc.vector.tensor_tensor(out=target, in0=source, in1=source, op=ALU.mult)
+
+        def quantise(pair, b):
+            grouped = grouped_of[(pair, b)]
             for half in range(2):
                 codes = packed.tile([P, HALF_PASSES * COLS], U32, align_bytes=64)
                 scales = packed.tile([P, HALF_PASSES * COLS], U8, align_bytes=64)
@@ -205,6 +214,13 @@ def tile_rgchromahistblock_k_kernel(tc, x, out):
                     scales=scales[:],
                     in_=grouped[:, half * HALF_PASSES : (half + 1) * HALF_PASSES].rearrange("p c g w j -> p (c g w j)"),
                 )
+                packed_of[(pair, b, half)] = (codes, scales)
+
+        def multiply(pair, b):
+            bank = hist_banks.tile([P, 512], F32)
+            bank_of[(pair, b)] = bank
+            for half in range(2):
+                codes, scales = packed_of[(pair, b, half)]
                 for c in range(HALF_PASSES):
                     cols = slice(c * COLS, (c + 1) * COLS)
                     nc.tensor.matmul_mx(
@@ -248,24 +264,41 @@ def tile_rgchromahistblock_k_kernel(tc, x, out):
             )
 
         pairs_of_group = GROUP // PAIR
+        slots = BINS // 4
+        fetch(0)
+        fetch(1)
         chroma(0)
-        prepare(0)
+        slopes(0)
+        for i in range(len(BASES)):
+            base_square(0, i)
+        pools.enter_context(tc.manual_schedule())
         for step in range(PAIRS + 3):
-            if step < PAIRS:
-                roots(step, 0)
-            if 1 <= step <= PAIRS:
-                values(step - 1, 1)
-                multiply(step - 1, 0)
-                multiply(step - 1, 1)
-            if step % LOADED_PAIRS == 0 and step + LOADED_PAIRS < PAIRS:
-                chroma(step // LOADED_PAIRS + 1)
-            if step + 1 < PAIRS:
-                prepare(step + 1)
-            if step < PAIRS:
-                roots(step, 1)
-                values(step, 0)
-            if 1 <= step <= PAIRS:
-                collect(step - 1, 0)
-                collect(step - 1, 1)
-            if 2 <= step and (step - 2) % pairs_of_group == pairs_of_group - 1:
-                normalise((step - 2) // pairs_of_group)
+            for half in range(2):
+                for slot in range(slots):
+                    if step < PAIRS:
+                        squares(step, half, slot)
+                        roots(step, half, slot)
+                        if step + 1 < PAIRS and slot % 3 == 2:
+                            base_square(step + 1, half * 5 + slot // 3)
+                    if half == 0 and slot in (2, 4) and 2 <= step <= PAIRS + 1:
+                        collect(step - 2, slot // 2 - 1)
+                    if half == 0 and 1 <= step <= PAIRS and slot % 2 == 0:
+                        values(step - 1, 1, slot // 2)
+                    if half == 1 and step < PAIRS and slot % 2 == 0:
+                        values(step, 0, slot // 2)
+                    if half == 1 and 1 <= step <= PAIRS and slot == slots // 2:
+                        multiply(step - 1, 0)
+                if half == 0:
+                    if 1 <= step <= PAIRS:
+                        quantise(step - 1, 0)
+                        quantise(step - 1, 1)
+                    if step % LOADED_PAIRS == 0 and step + LOADED_PAIRS < PAIRS:
+                        chroma(step // LOADED_PAIRS + 1)
+                        if step + 2 * LOADED_PAIRS < PAIRS:
+                            fetch(step // LOADED_PAIRS + 2)
+                    if step + 1 < PAIRS:
+                        slopes(step + 1)
+                elif 1 <= step <= PAIRS:
+                    multiply(step - 1, 1)
+            if 3 <= step and (step - 3) % pairs_of_group == pairs_of_group - 1:
+                normalise((step - 3) // pairs_of_group)

@@ -31,8 +31,8 @@ HALF_PASSES = PASSES // 2
 PAIR = 2
 PAIRS = IMAGES // PAIR
 LOADED_PAIRS = 2
-LOADED = PAIR * LOADED_PAIRS
 GROUP = 8
+GROUP_PAIRS = GROUP // PAIR
 LANES = 2 * PAIR * ROWS
 
 REACH = 3
@@ -80,13 +80,16 @@ def tile_rgchromahistblock_k_kernel(tc, x, out):
                 out=rest[:, j : j + 1], in0=one[:], scalar1=1.0 + 2.0 * t * (base_of(j) - MIDDLE) * STEP + t * t,
                 scalar2=0.0, op0=ALU.mult, op1=ALU.add,
             )
-        top_ones = const.tile([P, P], F32)
-        nc.vector.memset(top_ones[:], 0.0)
-        nc.vector.memset(top_ones[0:BINS, :], 1.0)
+        same_image = const.tile([P, P], F32)
+        nc.vector.memset(same_image[:], 0.0)
+        for b in range(PAIR):
+            half_range = slice(b * BINS, (b + 1) * BINS)
+            nc.vector.memset(same_image[half_range, half_range], 1.0)
         warm = const.tile([P, 1], F32)
         nc.scalar.activation(out=warm[:], in_=one[:], func=ACT.Abs_reciprocal_sqrt, bias=one[:], scale=1.0)
 
         raw_of = {}
+        inverse_of = {}
         minus_of = {}
         base_of_pair = {}
         slope_of_pair = {}
@@ -98,13 +101,12 @@ def tile_rgchromahistblock_k_kernel(tc, x, out):
         result_of = {}
 
         def image_of(pair, b):
-            return pair // LOADED_PAIRS * LOADED + b * LOADED_PAIRS + pair % LOADED_PAIRS
+            return pair // GROUP_PAIRS * GROUP + b * GROUP_PAIRS + pair % GROUP_PAIRS
 
         def fetch(load):
-            first = load * LOADED
             raw = inputs.tile([P, LOADED_PAIRS, CHANNELS, WIDTH], BF16)
             for b in range(PAIR):
-                start = first + b * LOADED_PAIRS
+                start = image_of(load * LOADED_PAIRS, b)
                 nc.sync.dma_start(
                     out=raw[b * ROWS : (b + 1) * ROWS],
                     in_=x[start : start + LOADED_PAIRS].rearrange("a c h w -> h a c w"),
@@ -122,12 +124,31 @@ def tile_rgchromahistblock_k_kernel(tc, x, out):
             nc.vector.scalar_tensor_tensor(
                 out=total[:], in0=clipped[:, :, 2, :], scalar=EPS, in1=total[:], op0=ALU.add, op1=ALU.add
             )
+            inverse_of[load] = (clipped, total)
+
+        def invert(load):
+            clipped, total = inverse_of[load]
             inverse = chroma_work.tile([P, LOADED_PAIRS, WIDTH], F32)
-            nc.vector.reciprocal(out=inverse[:], in_=total[:])
+            nc.scalar.activation(out=inverse[:], in_=total[:], func=ACT.Abs_reciprocal_sqrt)
+            nc.scalar.activation(out=inverse[:], in_=inverse[:], func=ACT.Square)
+            product = chroma_work.tile([P, LOADED_PAIRS, WIDTH], F32)
+            inverse_of[load] = (clipped, total, inverse, product)
+
+        def refine(load, part):
+            clipped, total, inverse, product = inverse_of[load]
+            if part == 0:
+                nc.vector.tensor_tensor(out=product[:], in0=total[:], in1=inverse[:], op=ALU.mult)
+            else:
+                nc.vector.scalar_tensor_tensor(
+                    out=inverse[:], in0=product[:], scalar=-2.0, in1=inverse[:], op0=ALU.add, op1=ALU.mult
+                )
+
+        def scale(load):
+            clipped, total, inverse, product = inverse_of[load]
             minus = lanes_pool.tile([P, LOADED_PAIRS, 2, WIDTH], F32)
             for channel in range(2):
                 nc.vector.scalar_tensor_tensor(
-                    out=minus[:, :, channel, :], in0=clipped[:, :, channel, :], scalar=-1.0 / SIGMA,
+                    out=minus[:, :, channel, :], in0=clipped[:, :, channel, :], scalar=1.0 / SIGMA,
                     in1=inverse[:], op0=ALU.mult, op1=ALU.mult,
                 )
             minus_of[load] = minus
@@ -190,84 +211,91 @@ def tile_rgchromahistblock_k_kernel(tc, x, out):
 
         def values(pair, half, unit):
             root = roots_of[(pair, half)]
-            b, channel, side = unit // 4, unit // 2 % 2, unit % 2
-            if half == 0 and (pair, b) not in grouped_of:
-                grouped = grouped_pool.tile([P, PASSES, 2, BINS, PACK], BF16, align_bytes=64)
-                grouped_of[(pair, b)] = grouped
-            grouped = grouped_of[(pair, b)]
+            channel, b, side = unit // 4, unit // 2 % 2, unit % 2
+            if (pair, channel) not in grouped_of:
+                grouped = grouped_pool.tile([P, PASSES, PAIR, BINS, PACK], BF16, align_bytes=64)
+                grouped_of[(pair, channel)] = grouped
+            grouped = grouped_of[(pair, channel)]
             low = (0, BINS - 16)[side] if half == 0 else (16, 32)[side]
             lane = channel * P + b * ROWS
             source = root[:, side * 16 : side * 16 + 16, lane : lane + ROWS].rearrange("p w (c j) -> p c w j", j=PACK)
-            target = grouped[:, :, channel, low : low + 16, :]
+            target = grouped[:, :, b, low : low + 16, :]
             if half == 0 and unit < SCALAR_UNITS:
                 nc.scalar.activation(out=target, in_=source, func=ACT.Square)
             else:
                 nc.vector.tensor_tensor(out=target, in0=source, in1=source, op=ALU.mult)
 
-        def quantise(pair, b):
-            grouped = grouped_of[(pair, b)]
+        def quantise(pair, channel):
+            grouped = grouped_of[(pair, channel)]
             for half in range(2):
                 codes = packed.tile([P, HALF_PASSES * COLS], U32, align_bytes=64)
                 scales = packed.tile([P, HALF_PASSES * COLS], U8, align_bytes=64)
                 nc.vector.quantize_mx(
                     out=codes[:].bitcast(FP8X4),
                     scales=scales[:],
-                    in_=grouped[:, half * HALF_PASSES : (half + 1) * HALF_PASSES].rearrange("p c g w j -> p (c g w j)"),
+                    in_=grouped[:, half * HALF_PASSES : (half + 1) * HALF_PASSES].rearrange("p c b w j -> p (c b w j)"),
                 )
-                packed_of[(pair, b, half)] = (codes, scales)
+                packed_of[(pair, channel, half)] = (codes, scales)
 
-        def multiply(pair, b):
+        def multiply(pair):
             bank = hist_banks.tile([P, 512], F32)
-            bank_of[(pair, b)] = bank
+            bank_of[pair] = bank
             for half in range(2):
-                codes, scales = packed_of[(pair, b, half)]
+                r_codes, r_scales = packed_of[(pair, 0, half)]
+                g_codes, g_scales = packed_of[(pair, 1, half)]
                 for c in range(HALF_PASSES):
                     cols = slice(c * COLS, (c + 1) * COLS)
                     nc.tensor.matmul_mx(
                         out=bank[:, 0:COLS],
-                        lhsT=codes[:, cols].bitcast(FP8X4),
-                        lhsT_scale=scales[:, cols],
-                        rhs=codes[:, cols].bitcast(FP8X4),
-                        rhs_scale=scales[:, cols],
+                        lhsT=r_codes[:, cols].bitcast(FP8X4),
+                        lhsT_scale=r_scales[:, cols],
+                        rhs=g_codes[:, cols].bitcast(FP8X4),
+                        rhs_scale=g_scales[:, cols],
                         start=(half == 0 and c == 0),
                         stop=(half == 1 and c == HALF_PASSES - 1),
                     )
 
-        def collect(pair, b):
-            image = image_of(pair, b)
-            group = image // GROUP
+        def collect(pair):
+            group = pair // GROUP_PAIRS
             if group not in result_of:
-                hist = results.tile([P, GROUP, BINS], F32)
-                row_sums = results.tile([P, GROUP], F32)
+                hist = results.tile([P, GROUP_PAIRS, BINS], F32)
+                row_sums = results.tile([P, GROUP_PAIRS], F32)
                 result_of[group] = (hist, row_sums)
             hist, row_sums = result_of[group]
-            i = image % GROUP
-            nc.scalar.activation(
-                out=hist[:, i, :], in_=bank_of[(pair, b)][:, BINS:COLS], func=ACT.Copy, accum_out=row_sums[:, i : i + 1]
-            )
+            i = pair % GROUP_PAIRS
+            for b in range(PAIR):
+                rows = slice(b * BINS, (b + 1) * BINS)
+                nc.scalar.activation(
+                    out=hist[rows, i, :], in_=bank_of[pair][rows, rows], func=ACT.Copy, accum_out=row_sums[rows, i : i + 1]
+                )
 
         def normalise(group):
             hist, row_sums = result_of[group]
-            sums = sum_banks.tile([P, GROUP], F32)
-            nc.tensor.matmul(out=sums[:], lhsT=top_ones[:], rhs=row_sums[:], start=True, stop=True)
-            divisor = results.tile([P, GROUP], F32)
+            sums = sum_banks.tile([P, GROUP_PAIRS], F32)
+            nc.tensor.matmul(out=sums[:], lhsT=same_image[:], rhs=row_sums[:], start=True, stop=True)
+            divisor = results.tile([P, GROUP_PAIRS], F32)
             nc.vector.tensor_scalar_add(out=divisor[:], in0=sums[:], scalar1=EPS)
-            factor = results.tile([P, GROUP], F32)
+            factor = results.tile([P, GROUP_PAIRS], F32)
             nc.vector.reciprocal(out=factor[:], in_=divisor[:])
-            normal = results.tile([P, GROUP, BINS], F32)
+            normal = results.tile([P, GROUP_PAIRS, BINS], F32)
             nc.vector.tensor_tensor(
-                out=normal[:], in0=hist[:], in1=factor[:].unsqueeze(2).to_broadcast([P, GROUP, BINS]), op=ALU.mult
+                out=normal[:], in0=hist[:], in1=factor[:].unsqueeze(2).to_broadcast([P, GROUP_PAIRS, BINS]), op=ALU.mult
             )
-            first = group * GROUP
-            nc.sync.dma_start(
-                out=out[first : first + GROUP].rearrange("b o i j -> i (b o) j"), in_=normal[0:BINS]
-            )
+            for b in range(PAIR):
+                first = image_of(group * GROUP_PAIRS, b)
+                nc.sync.dma_start(
+                    out=out[first : first + GROUP_PAIRS].rearrange("b o i j -> i (b o) j"),
+                    in_=normal[b * BINS : (b + 1) * BINS],
+                )
 
-        pairs_of_group = GROUP // PAIR
         slots = BINS // 4
         fetch(0)
         fetch(1)
         chroma(0)
+        invert(0)
+        refine(0, 0)
+        refine(0, 1)
+        scale(0)
         slopes(0)
         for i in range(len(BASES)):
             base_square(0, i)
@@ -280,14 +308,18 @@ def tile_rgchromahistblock_k_kernel(tc, x, out):
                         roots(step, half, slot)
                         if step + 1 < PAIRS and slot % 3 == 2:
                             base_square(step + 1, half * 5 + slot // 3)
-                    if half == 0 and slot in (2, 4) and 2 <= step <= PAIRS + 1:
-                        collect(step - 2, slot // 2 - 1)
+                    if half == 1 and slot == slots // 2 and step % LOADED_PAIRS == 0 and step + LOADED_PAIRS < PAIRS:
+                        invert(step // LOADED_PAIRS + 1)
+                    if half == 1 and slot in (12, 14) and step % LOADED_PAIRS == 0 and step + LOADED_PAIRS < PAIRS:
+                        refine(step // LOADED_PAIRS + 1, (slot - 12) // 2)
+                    if half == 0 and slot == 2 and 2 <= step <= PAIRS + 1:
+                        collect(step - 2)
                     if half == 0 and 1 <= step <= PAIRS and slot % 2 == 0:
                         values(step - 1, 1, slot // 2)
                     if half == 1 and step < PAIRS and slot % 2 == 0:
                         values(step, 0, slot // 2)
                     if half == 1 and 1 <= step <= PAIRS and slot == slots // 2:
-                        multiply(step - 1, 0)
+                        multiply(step - 1)
                 if half == 0:
                     if 1 <= step <= PAIRS:
                         quantise(step - 1, 0)
@@ -298,7 +330,7 @@ def tile_rgchromahistblock_k_kernel(tc, x, out):
                             fetch(step // LOADED_PAIRS + 2)
                     if step + 1 < PAIRS:
                         slopes(step + 1)
-                elif 1 <= step <= PAIRS:
-                    multiply(step - 1, 1)
-            if 3 <= step and (step - 3) % pairs_of_group == pairs_of_group - 1:
-                normalise((step - 3) // pairs_of_group)
+                elif step % LOADED_PAIRS == 0 and step + LOADED_PAIRS < PAIRS:
+                    scale(step // LOADED_PAIRS + 1)
+            if 3 <= step and (step - 3) % GROUP_PAIRS == GROUP_PAIRS - 1:
+                normalise((step - 3) // GROUP_PAIRS)

@@ -35,11 +35,11 @@ GROUP = 8
 GROUP_PAIRS = GROUP // PAIR
 LANES = 2 * PAIR * ROWS
 
-REACH = 3
+REACH = 4
 SPAN = 2 * REACH + 1
 LOW_BASES = list(range(0, BINS // 2, SPAN))
 BASES = LOW_BASES + [BINS - 1 - base for base in LOW_BASES]
-OFFSETS = [-3, -2, -1, 1, 2, 3]
+OFFSETS = [t for t in range(-REACH, REACH + 1) if t != 0]
 
 FLOPS = 2 * IMAGES * PIXELS * BINS * BINS
 
@@ -306,8 +306,8 @@ def tile_rgchromahistblock_k_kernel(tc, x, out):
                     if step < PAIRS:
                         squares(step, half, slot)
                         roots(step, half, slot)
-                        if step + 1 < PAIRS and slot % 3 == 2:
-                            base_square(step + 1, half * 5 + slot // 3)
+                        if step + 1 < PAIRS and slot % 4 == 3:
+                            base_square(step + 1, half * 4 + slot // 4)
                     if half == 1 and slot == slots // 2 and step % LOADED_PAIRS == 0 and step + LOADED_PAIRS < PAIRS:
                         invert(step // LOADED_PAIRS + 1)
                     if half == 1 and slot in (12, 14) and step % LOADED_PAIRS == 0 and step + LOADED_PAIRS < PAIRS:

@@ -73,6 +73,7 @@ def tile_rgchromahistblock_k_kernel(tc, x, out):
         nc.vector.memset(one[:], 1.0)
         identity = const.tile([P, P], F32)
         make_identity(nc, identity[:])
+        base = const.tile([P, len(BASES), LOADED_PAIRS, 2, WIDTH], F32)
         rest = const.tile([P, BINS // 2], F32)
         for j in range(BINS // 2):
             t = (j - base_of(j)) * STEP
@@ -91,14 +92,15 @@ def tile_rgchromahistblock_k_kernel(tc, x, out):
         raw_of = {}
         inverse_of = {}
         minus_of = {}
-        base_of_pair = {}
-        slope_of_pair = {}
+        slope_of = {}
         roots_of = {}
         grouped_of = {}
         bank_of = {}
         bank_of_squares = {}
         packed_of = {}
-        result_of = {}
+        hist_of = {}
+        row_sums_of = {}
+        sums_of = {}
 
         def image_of(pair, b):
             return pair // GROUP_PAIRS * GROUP + b * GROUP_PAIRS + pair % GROUP_PAIRS
@@ -153,32 +155,27 @@ def tile_rgchromahistblock_k_kernel(tc, x, out):
                 )
             minus_of[load] = minus
 
-        def source_of(pair):
-            return minus_of[pair // LOADED_PAIRS][:, pair % LOADED_PAIRS].rearrange("p g w -> p (g w)")
-
-        def slopes(pair):
-            slope = lanes_pool.tile([P, len(OFFSETS), 2, WIDTH], F32)
-            for i, t in enumerate(OFFSETS):
+        def slopes(load, part):
+            if part == 0:
+                slope = lanes_pool.tile([P, len(OFFSETS), LOADED_PAIRS, 2, WIDTH], F32)
+                slope_of[load] = slope
+            slope = slope_of[load]
+            for i in range(part * REACH, (part + 1) * REACH):
+                factor = 2.0 * OFFSETS[i] * STEP
                 nc.vector.tensor_scalar(
-                    out=slope[:, i].rearrange("p g w -> p (g w)"), in0=source_of(pair),
-                    scalar1=2.0 * t * STEP, scalar2=2.0 * t * STEP * MIDDLE * STEP, op0=ALU.mult, op1=ALU.add,
+                    out=slope[:, i].rearrange("p a g w -> p (a g w)"), in0=minus_of[load][:].rearrange("p a g w -> p (a g w)"),
+                    scalar1=factor, scalar2=factor * MIDDLE * STEP, op0=ALU.mult, op1=ALU.add,
                 )
-            slope_of_pair[pair] = slope
 
-        def base_square(pair, i):
-            if i == 0:
-                base = lanes_pool.tile([P, len(BASES), 2, WIDTH], F32)
-                base_of_pair[pair] = base
-            base = base_of_pair[pair]
-            j = BASES[i]
+        def base_square(load, i):
             nc.scalar.activation(
-                out=base[:, i].rearrange("p g w -> p (g w)"), in_=source_of(pair),
-                func=ACT.Square, bias=centre[:, j : j + 1], scale=1.0,
+                out=base[:, i].rearrange("p a g w -> p (a g w)"), in_=minus_of[load][:].rearrange("p a g w -> p (a g w)"),
+                func=ACT.Square, bias=centre[:, BASES[i] : BASES[i] + 1], scale=1.0,
             )
 
         def squares(pair, half, slot):
-            base = base_of_pair[pair]
-            slope = slope_of_pair[pair]
+            slope = slope_of[pair // LOADED_PAIRS]
+            a = pair % LOADED_PAIRS
             j = half * BINS // 4 + slot
             t = j - base_of(j)
             bank = squares_banks.tile([P, 2, 2, P], F32)
@@ -186,13 +183,13 @@ def tile_rgchromahistblock_k_kernel(tc, x, out):
                 for channel in range(2):
                     i = LOW_BASES.index(base_of(j)) + side * len(LOW_BASES)
                     nc.tensor.matmul(
-                        out=bank[:, side, channel, :], lhsT=base[:, i, channel, :], rhs=identity[:],
+                        out=bank[:, side, channel, :], lhsT=base[:, i, a, channel, :], rhs=identity[:],
                         is_transpose=True, start=True, stop=(t == 0),
                     )
                     if t != 0:
                         i = OFFSETS.index(t if side == 0 else -t)
                         nc.tensor.matmul(
-                            out=bank[:, side, channel, :], lhsT=slope[:, i, channel, :], rhs=identity[:],
+                            out=bank[:, side, channel, :], lhsT=slope[:, i, a, channel, :], rhs=identity[:],
                             is_transpose=True, start=False, stop=True,
                         )
             bank_of_squares[(pair, half, slot)] = bank
@@ -238,15 +235,18 @@ def tile_rgchromahistblock_k_kernel(tc, x, out):
                 packed_of[(pair, channel, half)] = (codes, scales)
 
         def multiply(pair):
-            bank = hist_banks.tile([P, 512], F32)
-            bank_of[pair] = bank
+            group = pair // GROUP_PAIRS
+            if group not in bank_of:
+                bank = hist_banks.tile([P, GROUP_PAIRS, COLS], F32)
+                bank_of[group] = bank
+            bank = bank_of[group]
             for half in range(2):
                 r_codes, r_scales = packed_of[(pair, 0, half)]
                 g_codes, g_scales = packed_of[(pair, 1, half)]
                 for c in range(HALF_PASSES):
                     cols = slice(c * COLS, (c + 1) * COLS)
                     nc.tensor.matmul_mx(
-                        out=bank[:, 0:COLS],
+                        out=bank[:, pair % GROUP_PAIRS, :],
                         lhsT=r_codes[:, cols].bitcast(FP8X4),
                         lhsT_scale=r_scales[:, cols],
                         rhs=g_codes[:, cols].bitcast(FP8X4),
@@ -255,31 +255,32 @@ def tile_rgchromahistblock_k_kernel(tc, x, out):
                         stop=(half == 1 and c == HALF_PASSES - 1),
                     )
 
-        def collect(pair):
-            group = pair // GROUP_PAIRS
-            if group not in result_of:
-                hist = results.tile([P, GROUP_PAIRS, BINS], F32)
-                row_sums = results.tile([P, GROUP_PAIRS], F32)
-                result_of[group] = (hist, row_sums)
-            hist, row_sums = result_of[group]
-            i = pair % GROUP_PAIRS
+        def collect(group):
+            hist = results.tile([P, GROUP_PAIRS, BINS], F32)
             for b in range(PAIR):
                 rows = slice(b * BINS, (b + 1) * BINS)
-                nc.scalar.activation(
-                    out=hist[rows, i, :], in_=bank_of[pair][rows, rows], func=ACT.Copy, accum_out=row_sums[rows, i : i + 1]
-                )
+                nc.scalar.copy(out=hist[rows], in_=bank_of[group][rows, :, rows])
+            hist_of[group] = hist
+
+        def add_rows(group):
+            row_sums = results.tile([P, GROUP_PAIRS], F32)
+            nc.vector.tensor_reduce(out=row_sums[:], in_=hist_of[group][:], op=ALU.add, axis=mybir.AxisListType.X)
+            row_sums_of[group] = row_sums
+
+        def add_images(group):
+            sums = sum_banks.tile([P, GROUP_PAIRS], F32)
+            nc.tensor.matmul(out=sums[:], lhsT=same_image[:], rhs=row_sums_of[group][:], start=True, stop=True)
+            sums_of[group] = sums
 
         def normalise(group):
-            hist, row_sums = result_of[group]
-            sums = sum_banks.tile([P, GROUP_PAIRS], F32)
-            nc.tensor.matmul(out=sums[:], lhsT=same_image[:], rhs=row_sums[:], start=True, stop=True)
+            sums = sums_of[group]
             divisor = results.tile([P, GROUP_PAIRS], F32)
             nc.vector.tensor_scalar_add(out=divisor[:], in0=sums[:], scalar1=EPS)
             factor = results.tile([P, GROUP_PAIRS], F32)
             nc.vector.reciprocal(out=factor[:], in_=divisor[:])
             normal = results.tile([P, GROUP_PAIRS, BINS], F32)
             nc.vector.tensor_tensor(
-                out=normal[:], in0=hist[:], in1=factor[:].unsqueeze(2).to_broadcast([P, GROUP_PAIRS, BINS]), op=ALU.mult
+                out=normal[:], in0=hist_of[group][:], in1=factor[:].unsqueeze(2).to_broadcast([P, GROUP_PAIRS, BINS]), op=ALU.mult
             )
             for b in range(PAIR):
                 first = image_of(group * GROUP_PAIRS, b)
@@ -296,9 +297,14 @@ def tile_rgchromahistblock_k_kernel(tc, x, out):
         refine(0, 0)
         refine(0, 1)
         scale(0)
-        slopes(0)
-        for i in range(len(BASES)):
+        slopes(0, 0)
+        slopes(0, 1)
+        for i in (0, 4, 1, 5, 2, 6):
             base_square(0, i)
+        base_at = {
+            (1, 0, 8): (1, 0), (1, 0, 12): (1, 4), (1, 1, 0): (1, 1), (1, 1, 3): (1, 5),
+            (1, 1, 9): (1, 2), (1, 1, 12): (1, 6), (0, 0, 3): (0, 3), (0, 0, 7): (0, 7),
+        }
         pools.enter_context(tc.manual_schedule())
         for step in range(PAIRS + 3):
             for half in range(2):
@@ -306,14 +312,16 @@ def tile_rgchromahistblock_k_kernel(tc, x, out):
                     if step < PAIRS:
                         squares(step, half, slot)
                         roots(step, half, slot)
-                        if step + 1 < PAIRS and slot % 4 == 3:
-                            base_square(step + 1, half * 4 + slot // 4)
+                    load, i = base_at.get((step % LOADED_PAIRS, half, slot), (0, None))
+                    load += step // LOADED_PAIRS
+                    if i is not None and load < PAIRS // LOADED_PAIRS:
+                        base_square(load, i)
                     if half == 1 and slot == slots // 2 and step % LOADED_PAIRS == 0 and step + LOADED_PAIRS < PAIRS:
                         invert(step // LOADED_PAIRS + 1)
                     if half == 1 and slot in (12, 14) and step % LOADED_PAIRS == 0 and step + LOADED_PAIRS < PAIRS:
                         refine(step // LOADED_PAIRS + 1, (slot - 12) // 2)
-                    if half == 0 and slot == 2 and 2 <= step <= PAIRS + 1:
-                        collect(step - 2)
+                    if half == 0 and slot == 2 and 2 <= step and (step - 2) % GROUP_PAIRS == GROUP_PAIRS - 1:
+                        collect((step - 2) // GROUP_PAIRS)
                     if half == 0 and 1 <= step <= PAIRS and slot % 2 == 0:
                         values(step - 1, 1, slot // 2)
                     if half == 1 and step < PAIRS and slot % 2 == 0:
@@ -328,9 +336,14 @@ def tile_rgchromahistblock_k_kernel(tc, x, out):
                         chroma(step // LOADED_PAIRS + 1)
                         if step + 2 * LOADED_PAIRS < PAIRS:
                             fetch(step // LOADED_PAIRS + 2)
-                    if step + 1 < PAIRS:
-                        slopes(step + 1)
-                elif step % LOADED_PAIRS == 0 and step + LOADED_PAIRS < PAIRS:
-                    scale(step // LOADED_PAIRS + 1)
-            if 3 <= step and (step - 3) % GROUP_PAIRS == GROUP_PAIRS - 1:
-                normalise((step - 3) // GROUP_PAIRS)
+                    if 2 <= step and (step - 2) % GROUP_PAIRS == GROUP_PAIRS - 1:
+                        add_rows((step - 2) // GROUP_PAIRS)
+                    if 3 <= step and (step - 3) % GROUP_PAIRS == GROUP_PAIRS - 1:
+                        normalise((step - 3) // GROUP_PAIRS)
+                else:
+                    if 2 <= step and (step - 2) % GROUP_PAIRS == GROUP_PAIRS - 1:
+                        add_images((step - 2) // GROUP_PAIRS)
+                    if step % LOADED_PAIRS == 0 and step + LOADED_PAIRS < PAIRS:
+                        scale(step // LOADED_PAIRS + 1)
+                if step % LOADED_PAIRS == 1 and step + 1 < PAIRS:
+                    slopes(step // LOADED_PAIRS + 1, half)

@@ -155,17 +155,16 @@ def tile_rgchromahistblock_k_kernel(tc, x, out):
                 )
             minus_of[load] = minus
 
-        def slopes(load, part):
-            if part == 0:
+        def slopes(load, i):
+            if i == 0:
                 slope = lanes_pool.tile([P, len(OFFSETS), LOADED_PAIRS, 2, WIDTH], F32)
                 slope_of[load] = slope
             slope = slope_of[load]
-            for i in range(part * REACH, (part + 1) * REACH):
-                factor = 2.0 * OFFSETS[i] * STEP
-                nc.vector.tensor_scalar(
-                    out=slope[:, i].rearrange("p a g w -> p (a g w)"), in0=minus_of[load][:].rearrange("p a g w -> p (a g w)"),
-                    scalar1=factor, scalar2=factor * MIDDLE * STEP, op0=ALU.mult, op1=ALU.add,
-                )
+            factor = 2.0 * OFFSETS[i] * STEP
+            nc.vector.tensor_scalar(
+                out=slope[:, i].rearrange("p a g w -> p (a g w)"), in0=minus_of[load][:].rearrange("p a g w -> p (a g w)"),
+                scalar1=factor, scalar2=factor * MIDDLE * STEP, op0=ALU.mult, op1=ALU.add,
+            )
 
         def base_square(load, i):
             nc.scalar.activation(
@@ -297,8 +296,8 @@ def tile_rgchromahistblock_k_kernel(tc, x, out):
         refine(0, 0)
         refine(0, 1)
         scale(0)
-        slopes(0, 0)
-        slopes(0, 1)
+        for i in range(len(OFFSETS)):
+            slopes(0, i)
         for i in (0, 4, 1, 5, 2, 6):
             base_square(0, i)
         base_at = {
@@ -316,6 +315,8 @@ def tile_rgchromahistblock_k_kernel(tc, x, out):
                     load += step // LOADED_PAIRS
                     if i is not None and load < PAIRS // LOADED_PAIRS:
                         base_square(load, i)
+                    if half == 0 and slot % 2 == 1 and step % LOADED_PAIRS == 1 and step + 1 < PAIRS:
+                        slopes(step // LOADED_PAIRS + 1, slot // 2)
                     if half == 1 and slot == slots // 2 and step % LOADED_PAIRS == 0 and step + LOADED_PAIRS < PAIRS:
                         invert(step // LOADED_PAIRS + 1)
                     if half == 1 and slot in (12, 14) and step % LOADED_PAIRS == 0 and step + LOADED_PAIRS < PAIRS:
@@ -345,5 +346,3 @@ def tile_rgchromahistblock_k_kernel(tc, x, out):
                         add_images((step - 2) // GROUP_PAIRS)
                     if step % LOADED_PAIRS == 0 and step + LOADED_PAIRS < PAIRS:
                         scale(step // LOADED_PAIRS + 1)
-                if step % LOADED_PAIRS == 1 and step + 1 < PAIRS:
-                    slopes(step // LOADED_PAIRS + 1, half)

@@ -43,8 +43,6 @@ OFFSETS = [t for t in range(-REACH, REACH + 1) if t != 0]
 
 FLOPS = 2 * IMAGES * PIXELS * BINS * BINS
 
-SCALAR_UNITS = 1
-
 
 def base_of(bin_number):
     return (bin_number + REACH) // SPAN * SPAN
@@ -102,6 +100,9 @@ def tile_rgchromahistblock_k_kernel(tc, x, out):
         row_sums_of = {}
         sums_of = {}
 
+        def scalar_units(pair):
+            return 2 if pair % 4 == 0 else 1
+
         def image_of(pair, b):
             return pair // GROUP_PAIRS * GROUP + b * GROUP_PAIRS + pair % GROUP_PAIRS
 
@@ -117,7 +118,7 @@ def tile_rgchromahistblock_k_kernel(tc, x, out):
 
         def chroma(load):
             raw = raw_of[load]
-            clipped = chroma_work.tile([P, LOADED_PAIRS, CHANNELS, WIDTH], F32)
+            clipped = chroma_work.tile([P, LOADED_PAIRS, CHANNELS, WIDTH], BF16)
             nc.vector.tensor_scalar(
                 out=clipped[:], in0=raw[:], scalar1=0.0, scalar2=1.0, op0=ALU.max, op1=ALU.min
             )
@@ -205,18 +206,17 @@ def tile_rgchromahistblock_k_kernel(tc, x, out):
                 func=ACT.Abs_reciprocal_sqrt, bias=rest[:, j : j + 1], scale=1.0,
             )
 
-        def values(pair, half, unit):
-            root = roots_of[(pair, half)]
-            channel, b, side = unit // 4, unit // 2 % 2, unit % 2
+        def values(pair, half, channel, b, first, count, engine):
             if (pair, channel) not in grouped_of:
                 grouped = grouped_pool.tile([P, PASSES, PAIR, BINS, PACK], BF16, align_bytes=64)
                 grouped_of[(pair, channel)] = grouped
-            grouped = grouped_of[(pair, channel)]
-            low = (0, BINS - 16)[side] if half == 0 else (16, 32)[side]
+            low = first + (BINS // 4 if half == 1 else 0 if first < BINS // 4 else BINS // 2)
             lane = channel * P + b * ROWS
-            source = root[:, side * 16 : side * 16 + 16, lane : lane + ROWS].rearrange("p w (c j) -> p c w j", j=PACK)
-            target = grouped[:, :, b, low : low + 16, :]
-            if half == 0 and unit < SCALAR_UNITS:
+            source = roots_of[(pair, half)][:, first : first + count, lane : lane + ROWS].rearrange(
+                "p w (c j) -> p c w j", j=PACK
+            )
+            target = grouped_of[(pair, channel)][:, :, b, low : low + count, :]
+            if engine is nc.scalar:
                 nc.scalar.activation(out=target, in_=source, func=ACT.Square)
             else:
                 nc.vector.tensor_tensor(out=target, in0=source, in1=source, op=ALU.mult)
@@ -298,8 +298,12 @@ def tile_rgchromahistblock_k_kernel(tc, x, out):
         scale(0)
         for i in range(len(OFFSETS)):
             slopes(0, i)
-        for i in (0, 4, 1, 5, 2, 6):
-            base_square(0, i)
+        base_square(0, 0)
+        base_square(0, 4)
+        shifted = chroma_work.tile([P, LOADED_PAIRS, 2, WIDTH], F32)
+        for i in (1, 5, 2, 6, 3, 7):
+            nc.vector.tensor_scalar_add(out=shifted[:], in0=minus_of[0][:], scalar1=BASES[i] * STEP)
+            nc.vector.tensor_tensor(out=base[:, i], in0=shifted[:], in1=shifted[:], op=ALU.mult)
         base_at = {
             (1, 0, 8): (1, 0), (1, 0, 12): (1, 4), (1, 1, 0): (1, 1), (1, 1, 3): (1, 5),
             (1, 1, 9): (1, 2), (1, 1, 12): (1, 6), (0, 0, 3): (0, 3), (0, 0, 7): (0, 7),
@@ -313,7 +317,7 @@ def tile_rgchromahistblock_k_kernel(tc, x, out):
                         roots(step, half, slot)
                     load, i = base_at.get((step % LOADED_PAIRS, half, slot), (0, None))
                     load += step // LOADED_PAIRS
-                    if i is not None and load < PAIRS // LOADED_PAIRS:
+                    if i is not None and 0 < load < PAIRS // LOADED_PAIRS:
                         base_square(load, i)
                     if half == 0 and slot % 2 == 1 and step % LOADED_PAIRS == 1 and step + 1 < PAIRS:
                         slopes(step // LOADED_PAIRS + 1, slot // 2)
@@ -323,10 +327,22 @@ def tile_rgchromahistblock_k_kernel(tc, x, out):
                         refine(step // LOADED_PAIRS + 1, (slot - 12) // 2)
                     if half == 0 and slot == 2 and 2 <= step and (step - 2) % GROUP_PAIRS == GROUP_PAIRS - 1:
                         collect((step - 2) // GROUP_PAIRS)
-                    if half == 0 and 1 <= step <= PAIRS and slot % 2 == 0:
-                        values(step - 1, 1, slot // 2)
-                    if half == 1 and step < PAIRS and slot % 2 == 0:
-                        values(step, 0, slot // 2)
+                    if half == 0 and 1 <= step <= PAIRS and slot % 4 == 0:
+                        channel, b = slot // 8, slot // 4 % 2
+                        engine = nc.scalar if step == PAIRS and channel == 1 else nc.vector
+                        values(step - 1, 1, channel, b, 0, BINS // 2, engine)
+                    if half == 0 and step == 0 and slot == slots // 2 - 1:
+                        for channel in range(2):
+                            for b in range(PAIR):
+                                values(0, 0, channel, b, 0, 8, nc.vector)
+                                values(0, 0, channel, b, 24, 8, nc.vector)
+                    if half == 1 and step == 0 and slot % 4 == 0:
+                        values(0, 0, slot // 8, slot // 4 % 2, 8, 8, nc.vector)
+                        values(0, 0, slot // 8, slot // 4 % 2, 16, 8, nc.vector)
+                    if half == 1 and 1 <= step < PAIRS and slot % 2 == 0:
+                        unit = slot // 2
+                        engine = nc.scalar if unit < scalar_units(step) else nc.vector
+                        values(step, 0, unit // 4, unit // 2 % 2, unit % 2 * 16, 16, engine)
                     if half == 1 and 1 <= step <= PAIRS and slot == slots // 2:
                         multiply(step - 1)
                 if half == 0:

@@ -48,6 +48,11 @@ def base_of(bin_number):
     return (bin_number + REACH) // SPAN * SPAN
 
 
+def rest_of(bin_number):
+    offset = (bin_number - base_of(bin_number)) * STEP
+    return 1.0 + 2.0 * offset * (base_of(bin_number) - MIDDLE) * STEP + offset * offset
+
+
 def tile_rgchromahistblock_k_kernel(tc, x, out):
     nc = tc.nc
     with ExitStack() as pools:
@@ -59,8 +64,8 @@ def tile_rgchromahistblock_k_kernel(tc, x, out):
         grouped_pool = pools.enter_context(tc.tile_pool(name="grouped_pool", bufs=3))
         packed = pools.enter_context(tc.tile_pool(name="packed", bufs=4))
         results = pools.enter_context(tc.tile_pool(name="results", bufs=2))
-        squares_banks = pools.enter_context(tc.psum_pool(name="squares_banks", bufs=5))
-        hist_banks = pools.enter_context(tc.psum_pool(name="hist_banks", bufs=2))
+        squares_banks = pools.enter_context(tc.psum_pool(name="squares_banks", bufs=6))
+        hist_banks = pools.enter_context(tc.psum_pool(name="hist_banks", bufs=1))
         sum_banks = pools.enter_context(tc.psum_pool(name="sum_banks", bufs=1))
 
         bin_number = const.tile([P, BINS], I32)
@@ -69,16 +74,9 @@ def tile_rgchromahistblock_k_kernel(tc, x, out):
         nc.vector.tensor_scalar_mul(out=centre[:], in0=bin_number[:], scalar1=STEP)
         one = const.tile([P, 1], F32)
         nc.vector.memset(one[:], 1.0)
-        identity = const.tile([P, P], F32)
+        identity = const.tile([P, P], F32, align_bytes=256)
         make_identity(nc, identity[:])
-        base = const.tile([P, len(BASES), LOADED_PAIRS, 2, WIDTH], F32)
-        rest = const.tile([P, BINS // 2], F32)
-        for j in range(BINS // 2):
-            t = (j - base_of(j)) * STEP
-            nc.gpsimd.tensor_scalar(
-                out=rest[:, j : j + 1], in0=one[:], scalar1=1.0 + 2.0 * t * (base_of(j) - MIDDLE) * STEP + t * t,
-                scalar2=0.0, op0=ALU.mult, op1=ALU.add,
-            )
+        base = const.tile([P, len(BASES), LOADED_PAIRS, 2, WIDTH], F32, align_bytes=256)
         same_image = const.tile([P, P], F32)
         nc.vector.memset(same_image[:], 0.0)
         for b in range(PAIR):
@@ -101,7 +99,7 @@ def tile_rgchromahistblock_k_kernel(tc, x, out):
         sums_of = {}
 
         def scalar_units(pair):
-            return 2 if pair % 4 == 0 else 1
+            return 1
 
         def image_of(pair, b):
             return pair // GROUP_PAIRS * GROUP + b * GROUP_PAIRS + pair % GROUP_PAIRS
@@ -158,7 +156,7 @@ def tile_rgchromahistblock_k_kernel(tc, x, out):
 
         def slopes(load, i):
             if i == 0:
-                slope = lanes_pool.tile([P, len(OFFSETS), LOADED_PAIRS, 2, WIDTH], F32)
+                slope = lanes_pool.tile([P, len(OFFSETS), LOADED_PAIRS, 2, WIDTH], F32, align_bytes=256)
                 slope_of[load] = slope
             slope = slope_of[load]
             factor = 2.0 * OFFSETS[i] * STEP
@@ -203,7 +201,7 @@ def tile_rgchromahistblock_k_kernel(tc, x, out):
             nc.scalar.activation(
                 out=root[:, slot : BINS // 2 - slot : BINS // 2 - 1 - 2 * slot, :],
                 in_=bank_of_squares[(pair, half, slot)][:].rearrange("p s c l -> p s (c l)"),
-                func=ACT.Abs_reciprocal_sqrt, bias=rest[:, j : j + 1], scale=1.0,
+                func=ACT.Abs_reciprocal_sqrt, bias=rest_of(j), scale=1.0,
             )
 
         def values(pair, half, channel, b, first, count, engine):

@@ -99,7 +99,7 @@ def tile_rgchromahistblock_k_kernel(tc, x, out):
         sums_of = {}
 
         def scalar_units(pair):
-            return 1
+            return 2 - pair % LOADED_PAIRS
 
         def image_of(pair, b):
             return pair // GROUP_PAIRS * GROUP + b * GROUP_PAIRS + pair % GROUP_PAIRS

from contextlib import ExitStack

import concourse.mybir as mybir
from concourse.masks import make_identity

F32 = mybir.dt.float32
BF16 = mybir.dt.bfloat16
I32 = mybir.dt.int32
U32 = mybir.dt.uint32
U8 = mybir.dt.uint8
FP8X4 = mybir.dt.float8_e4m3fn_x4
ALU = mybir.AluOpType
ACT = mybir.ActivationFunctionType

P = 128
IMAGES = 128
CHANNELS = 3
ROWS = 64
WIDTH = 128
PIXELS = ROWS * WIDTH
BINS = 64
EPS = 1e-6
SIGMA = 0.02
STEP = 1.0 / ((BINS - 1) * SIGMA)
MIDDLE = (BINS - 1) / 2.0

PACK = 4
PASSES = ROWS // PACK
COLS = 2 * BINS
HALF_PASSES = PASSES // 2
PAIR = 2
PAIRS = IMAGES // PAIR
LOADED_PAIRS = 2
GROUP = 8
GROUP_PAIRS = GROUP // PAIR
LANES = 2 * PAIR * ROWS

REACH = 4
SPAN = 2 * REACH + 1
LOW_BASES = list(range(0, BINS // 2, SPAN))
BASES = LOW_BASES + [BINS - 1 - base for base in LOW_BASES]
OFFSETS = [t for t in range(-REACH, REACH + 1) if t != 0]

FLOPS = 2 * IMAGES * PIXELS * BINS * BINS


def base_of(bin_number):
    return (bin_number + REACH) // SPAN * SPAN


def rest_of(bin_number):
    offset = (bin_number - base_of(bin_number)) * STEP
    return 1.0 + 2.0 * offset * (base_of(bin_number) - MIDDLE) * STEP + offset * offset


def tile_rgchromahistblock_k_kernel(tc, x, out):
    nc = tc.nc
    with ExitStack() as pools:
        const = pools.enter_context(tc.tile_pool(name="const", bufs=1))
        inputs = pools.enter_context(tc.tile_pool(name="inputs", bufs=2))
        chroma_work = pools.enter_context(tc.tile_pool(name="chroma_work", bufs=1))
        lanes_pool = pools.enter_context(tc.tile_pool(name="lanes_pool", bufs=2))
        wide = pools.enter_context(tc.tile_pool(name="wide", bufs=3))
        grouped_pool = pools.enter_context(tc.tile_pool(name="grouped_pool", bufs=3))
        packed = pools.enter_context(tc.tile_pool(name="packed", bufs=4))
        results = pools.enter_context(tc.tile_pool(name="results", bufs=2))
        squares_banks = pools.enter_context(tc.psum_pool(name="squares_banks", bufs=6))
        hist_banks = pools.enter_context(tc.psum_pool(name="hist_banks", bufs=1))
        sum_banks = pools.enter_context(tc.psum_pool(name="sum_banks", bufs=1))

        bin_number = const.tile([P, BINS], I32)
        nc.gpsimd.iota(bin_number[:], pattern=[[1, BINS]], base=0, channel_multiplier=0)
        centre = const.tile([P, BINS], F32)
        nc.vector.tensor_scalar_mul(out=centre[:], in0=bin_number[:], scalar1=STEP)
        one = const.tile([P, 1], F32)
        nc.vector.memset(one[:], 1.0)
        identity = const.tile([P, P], F32, align_bytes=256)
        make_identity(nc, identity[:])
        base = const.tile([P, len(BASES), LOADED_PAIRS, 2, WIDTH], F32, align_bytes=256)
        same_image = const.tile([P, P], F32)
        nc.vector.memset(same_image[:], 0.0)
        for b in range(PAIR):
            half_range = slice(b * BINS, (b + 1) * BINS)
            nc.vector.memset(same_image[half_range, half_range], 1.0)
        warm = const.tile([P, 1], F32)
        nc.scalar.activation(out=warm[:], in_=one[:], func=ACT.Abs_reciprocal_sqrt, bias=one[:], scale=1.0)

        raw_of = {}
        inverse_of = {}
        minus_of = {}
        slope_of = {}
        roots_of = {}
        grouped_of = {}
        bank_of = {}
        bank_of_squares = {}
        packed_of = {}
        hist_of = {}
        row_sums_of = {}
        sums_of = {}

        def scalar_units(pair):
            return 2 - pair % LOADED_PAIRS

        def image_of(pair, b):
            return pair // GROUP_PAIRS * GROUP + b * GROUP_PAIRS + pair % GROUP_PAIRS

        def fetch(load):
            raw = inputs.tile([P, LOADED_PAIRS, CHANNELS, WIDTH], BF16)
            for b in range(PAIR):
                start = image_of(load * LOADED_PAIRS, b)
                nc.sync.dma_start(
                    out=raw[b * ROWS : (b + 1) * ROWS],
                    in_=x[start : start + LOADED_PAIRS].rearrange("a c h w -> h a c w"),
                )
            raw_of[load] = raw

        def chroma(load):
            raw = raw_of[load]
            clipped = chroma_work.tile([P, LOADED_PAIRS, CHANNELS, WIDTH], BF16)
            nc.vector.tensor_scalar(
                out=clipped[:], in0=raw[:], scalar1=0.0, scalar2=1.0, op0=ALU.max, op1=ALU.min
            )
            total = chroma_work.tile([P, LOADED_PAIRS, WIDTH], F32)
            nc.vector.tensor_tensor(out=total[:], in0=clipped[:, :, 0, :], in1=clipped[:, :, 1, :], op=ALU.add)
            nc.vector.scalar_tensor_tensor(
                out=total[:], in0=clipped[:, :, 2, :], scalar=EPS, in1=total[:], op0=ALU.add, op1=ALU.add
            )
            inverse_of[load] = (clipped, total)

        def invert(load):
            clipped, total = inverse_of[load]
            inverse = chroma_work.tile([P, LOADED_PAIRS, WIDTH], F32)
            nc.scalar.activation(out=inverse[:], in_=total[:], func=ACT.Abs_reciprocal_sqrt)
            nc.scalar.activation(out=inverse[:], in_=inverse[:], func=ACT.Square)
            product = chroma_work.tile([P, LOADED_PAIRS, WIDTH], F32)
            inverse_of[load] = (clipped, total, inverse, product)

        def refine(load, part):
            clipped, total, inverse, product = inverse_of[load]
            if part == 0:
                nc.vector.tensor_tensor(out=product[:], in0=total[:], in1=inverse[:], op=ALU.mult)
            else:
                nc.vector.scalar_tensor_tensor(
                    out=inverse[:], in0=product[:], scalar=-2.0, in1=inverse[:], op0=ALU.add, op1=ALU.mult
                )

        def scale(load):
            clipped, total, inverse, product = inverse_of[load]
            minus = lanes_pool.tile([P, LOADED_PAIRS, 2, WIDTH], F32)
            for channel in range(2):
                nc.vector.scalar_tensor_tensor(
                    out=minus[:, :, channel, :], in0=clipped[:, :, channel, :], scalar=1.0 / SIGMA,
                    in1=inverse[:], op0=ALU.mult, op1=ALU.mult,
                )
            minus_of[load] = minus

        def slopes(load, i):
            if i == 0:
                slope = lanes_pool.tile([P, len(OFFSETS), LOADED_PAIRS, 2, WIDTH], F32, align_bytes=256)
                slope_of[load] = slope
            slope = slope_of[load]
            factor = 2.0 * OFFSETS[i] * STEP
            nc.vector.tensor_scalar(
                out=slope[:, i].rearrange("p a g w -> p (a g w)"), in0=minus_of[load][:].rearrange("p a g w -> p (a g w)"),
                scalar1=factor, scalar2=factor * MIDDLE * STEP, op0=ALU.mult, op1=ALU.add,
            )

        def base_square(load, i):
            nc.scalar.activation(
                out=base[:, i].rearrange("p a g w -> p (a g w)"), in_=minus_of[load][:].rearrange("p a g w -> p (a g w)"),
                func=ACT.Square, bias=centre[:, BASES[i] : BASES[i] + 1], scale=1.0,
            )

        def squares(pair, half, slot):
            slope = slope_of[pair // LOADED_PAIRS]
            a = pair % LOADED_PAIRS
            j = half * BINS // 4 + slot
            t = j - base_of(j)
            bank = squares_banks.tile([P, 2, 2, P], F32)
            for side in range(2):
                for channel in range(2):
                    i = LOW_BASES.index(base_of(j)) + side * len(LOW_BASES)
                    nc.tensor.matmul(
                        out=bank[:, side, channel, :], lhsT=base[:, i, a, channel, :], rhs=identity[:],
                        is_transpose=True, start=True, stop=(t == 0),
                    )
                    if t != 0:
                        i = OFFSETS.index(t if side == 0 else -t)
                        nc.tensor.matmul(
                            out=bank[:, side, channel, :], lhsT=slope[:, i, a, channel, :], rhs=identity[:],
                            is_transpose=True, start=False, stop=True,
                        )
            bank_of_squares[(pair, half, slot)] = bank

        def roots(pair, half, slot):
            if slot == 0:
                root = wide.tile([P, BINS // 2, LANES], F32)
                roots_of[(pair, half)] = root
            root = roots_of[(pair, half)]
            j = half * BINS // 4 + slot
            nc.scalar.activation(
                out=root[:, slot : BINS // 2 - slot : BINS // 2 - 1 - 2 * slot, :],
                in_=bank_of_squares[(pair, half, slot)][:].rearrange("p s c l -> p s (c l)"),
                func=ACT.Abs_reciprocal_sqrt, bias=rest_of(j), scale=1.0,
            )

        def values(pair, half, channel, b, first, count, engine):
            if (pair, channel) not in grouped_of:
                grouped = grouped_pool.tile([P, PASSES, PAIR, BINS, PACK], BF16, align_bytes=64)
                grouped_of[(pair, channel)] = grouped
            low = first + (BINS // 4 if half == 1 else 0 if first < BINS // 4 else BINS // 2)
            lane = channel * P + b * ROWS
            source = roots_of[(pair, half)][:, first : first + count, lane : lane + ROWS].rearrange(
                "p w (c j) -> p c w j", j=PACK
            )
            target = grouped_of[(pair, channel)][:, :, b, low : low + count, :]
            if engine is nc.scalar:
                nc.scalar.activation(out=target, in_=source, func=ACT.Square)
            else:
                nc.vector.tensor_tensor(out=target, in0=source, in1=source, op=ALU.mult)

        def quantise(pair, channel):
            grouped = grouped_of[(pair, channel)]
            for half in range(2):
                codes = packed.tile([P, HALF_PASSES * COLS], U32, align_bytes=64)
                scales = packed.tile([P, HALF_PASSES * COLS], U8, align_bytes=64)
                nc.vector.quantize_mx(
                    out=codes[:].bitcast(FP8X4),
                    scales=scales[:],
                    in_=grouped[:, half * HALF_PASSES : (half + 1) * HALF_PASSES].rearrange("p c b w j -> p (c b w j)"),
                )
                packed_of[(pair, channel, half)] = (codes, scales)

        def multiply(pair):
            group = pair // GROUP_PAIRS
            if group not in bank_of:
                bank = hist_banks.tile([P, GROUP_PAIRS, COLS], F32)
                bank_of[group] = bank
            bank = bank_of[group]
            for half in range(2):
                r_codes, r_scales = packed_of[(pair, 0, half)]
                g_codes, g_scales = packed_of[(pair, 1, half)]
                for c in range(HALF_PASSES):
                    cols = slice(c * COLS, (c + 1) * COLS)
                    nc.tensor.matmul_mx(
                        out=bank[:, pair % GROUP_PAIRS, :],
                        lhsT=r_codes[:, cols].bitcast(FP8X4),
                        lhsT_scale=r_scales[:, cols],
                        rhs=g_codes[:, cols].bitcast(FP8X4),
                        rhs_scale=g_scales[:, cols],
                        start=(half == 0 and c == 0),
                        stop=(half == 1 and c == HALF_PASSES - 1),
                    )

        def collect(group):
            hist = results.tile([P, GROUP_PAIRS, BINS], F32)
            for b in range(PAIR):
                rows = slice(b * BINS, (b + 1) * BINS)
                nc.scalar.copy(out=hist[rows], in_=bank_of[group][rows, :, rows])
            hist_of[group] = hist

        def add_rows(group):
            row_sums = results.tile([P, GROUP_PAIRS], F32)
            nc.vector.tensor_reduce(out=row_sums[:], in_=hist_of[group][:], op=ALU.add, axis=mybir.AxisListType.X)
            row_sums_of[group] = row_sums

        def add_images(group):
            sums = sum_banks.tile([P, GROUP_PAIRS], F32)
            nc.tensor.matmul(out=sums[:], lhsT=same_image[:], rhs=row_sums_of[group][:], start=True, stop=True)
            sums_of[group] = sums

        def normalise(group):
            sums = sums_of[group]
            divisor = results.tile([P, GROUP_PAIRS], F32)
            nc.vector.tensor_scalar_add(out=divisor[:], in0=sums[:], scalar1=EPS)
            factor = results.tile([P, GROUP_PAIRS], F32)
            nc.vector.reciprocal(out=factor[:], in_=divisor[:])
            normal = results.tile([P, GROUP_PAIRS, BINS], F32)
            nc.vector.tensor_tensor(
                out=normal[:], in0=hist_of[group][:], in1=factor[:].unsqueeze(2).to_broadcast([P, GROUP_PAIRS, BINS]), op=ALU.mult
            )
            for b in range(PAIR):
                first = image_of(group * GROUP_PAIRS, b)
                nc.sync.dma_start(
                    out=out[first : first + GROUP_PAIRS].rearrange("b o i j -> i (b o) j"),
                    in_=normal[b * BINS : (b + 1) * BINS],
                )

        slots = BINS // 4
        fetch(0)
        fetch(1)
        chroma(0)
        invert(0)
        refine(0, 0)
        refine(0, 1)
        scale(0)
        for i in range(len(OFFSETS)):
            slopes(0, i)
        base_square(0, 0)
        base_square(0, 4)
        shifted = chroma_work.tile([P, LOADED_PAIRS, 2, WIDTH], F32)
        for i in (1, 5, 2, 6, 3, 7):
            nc.vector.tensor_scalar_add(out=shifted[:], in0=minus_of[0][:], scalar1=BASES[i] * STEP)
            nc.vector.tensor_tensor(out=base[:, i], in0=shifted[:], in1=shifted[:], op=ALU.mult)
        base_at = {
            (1, 0, 8): (1, 0), (1, 0, 12): (1, 4), (1, 1, 0): (1, 1), (1, 1, 3): (1, 5),
            (1, 1, 9): (1, 2), (1, 1, 12): (1, 6), (0, 0, 3): (0, 3), (0, 0, 7): (0, 7),
        }
        pools.enter_context(tc.manual_schedule())
        for step in range(PAIRS + 3):
            for half in range(2):
                for slot in range(slots):
                    if step < PAIRS:
                        squares(step, half, slot)
                        roots(step, half, slot)
                    load, i = base_at.get((step % LOADED_PAIRS, half, slot), (0, None))
                    load += step // LOADED_PAIRS
                    if i is not None and 0 < load < PAIRS // LOADED_PAIRS:
                        base_square(load, i)
                    if half == 0 and slot % 2 == 1 and step % LOADED_PAIRS == 1 and step + 1 < PAIRS:
                        slopes(step // LOADED_PAIRS + 1, slot // 2)
                    if half == 1 and slot == slots // 2 and step % LOADED_PAIRS == 0 and step + LOADED_PAIRS < PAIRS:
                        invert(step // LOADED_PAIRS + 1)
                    if half == 1 and slot in (12, 14) and step % LOADED_PAIRS == 0 and step + LOADED_PAIRS < PAIRS:
                        refine(step // LOADED_PAIRS + 1, (slot - 12) // 2)
                    if half == 0 and slot == 2 and 2 <= step and (step - 2) % GROUP_PAIRS == GROUP_PAIRS - 1:
                        collect((step - 2) // GROUP_PAIRS)
                    if half == 0 and 1 <= step <= PAIRS and slot % 4 == 0:
                        channel, b = slot // 8, slot // 4 % 2
                        engine = nc.scalar if step == PAIRS and channel == 1 else nc.vector
                        values(step - 1, 1, channel, b, 0, BINS // 2, engine)
                    if half == 0 and step == 0 and slot == slots // 2 - 1:
                        for channel in range(2):
                            for b in range(PAIR):
                                values(0, 0, channel, b, 0, 8, nc.vector)
                                values(0, 0, channel, b, 24, 8, nc.vector)
                    if half == 1 and step == 0 and slot % 4 == 0:
                        values(0, 0, slot // 8, slot // 4 % 2, 8, 8, nc.vector)
                        values(0, 0, slot // 8, slot // 4 % 2, 16, 8, nc.vector)
                    if half == 1 and 1 <= step < PAIRS and slot % 2 == 0:
                        unit = slot // 2
                        engine = nc.scalar if unit < scalar_units(step) else nc.vector
                        values(step, 0, unit // 4, unit // 2 % 2, unit % 2 * 16, 16, engine)
                    if half == 1 and 1 <= step <= PAIRS and slot == slots // 2:
                        multiply(step - 1)
                if half == 0:
                    if 1 <= step <= PAIRS:
                        quantise(step - 1, 0)
                        quantise(step - 1, 1)
                    if step % LOADED_PAIRS == 0 and step + LOADED_PAIRS < PAIRS:
                        chroma(step // LOADED_PAIRS + 1)
                        if step + 2 * LOADED_PAIRS < PAIRS:
                            fetch(step // LOADED_PAIRS + 2)
                    if 2 <= step and (step - 2) % GROUP_PAIRS == GROUP_PAIRS - 1:
                        add_rows((step - 2) // GROUP_PAIRS)
                    if 3 <= step and (step - 3) % GROUP_PAIRS == GROUP_PAIRS - 1:
                        normalise((step - 3) // GROUP_PAIRS)
                else:
                    if 2 <= step and (step - 2) % GROUP_PAIRS == GROUP_PAIRS - 1:
                        add_images((step - 2) // GROUP_PAIRS)
                    if step % LOADED_PAIRS == 0 and step + LOADED_PAIRS < PAIRS:
                        scale(step // LOADED_PAIRS + 1)
